import numpy as np
import ml_dtypes


def mxq(x, axis, fmt="e4m3"):
    dtype, down = {"e4m3": (ml_dtypes.float8_e4m3fn, 7), "e5m2": (ml_dtypes.float8_e5m2, 14)}[fmt]
    v = np.moveaxis(np.asarray(x, np.float32).astype(ml_dtypes.bfloat16).astype(np.float64), axis, -1)
    blocks = v.reshape(v.shape[:-1] + (-1, 32))
    amax = np.abs(blocks).max(-1, keepdims=True)
    byte = np.maximum(np.where(amax > 0, np.frexp(amax)[1] - 1 + 127, 0) - down, 1)
    scale = np.exp2(byte - 127.0)
    codes = (blocks / scale).astype(np.float32).astype(dtype).astype(np.float64)
    return np.moveaxis((codes * scale).reshape(v.shape), -1, axis)


WIDE = False


def mx_kscale(k):
    if not WIDE:
        return np.ones(k)
    levels = np.array([10, -10, 5, -5, 0])
    a = np.random.permutation(np.resize(levels, k // 512 * 4)).reshape(k // 512, 4)
    idx = np.arange(k)
    return np.exp2(a[idx // 512, idx % 128 // 32])


BF16 = ml_dtypes.bfloat16


def bf(x):
    return np.asarray(x, np.float32).astype(BF16)


def f64(x):
    return np.asarray(x).astype(np.float64)


E2M1 = np.array([0.0, 0.5, 1.0, 1.5, 2.0, 3.0, 4.0, 6.0, -0.0, -0.5, -1.0, -1.5, -2.0, -3.0, -4.0, -6.0])


def pack_weight(w, fmt):
    k, n = w.shape
    w = f64(bf(w)).reshape(k // 32, 32, n)
    amax = np.abs(w).max(1)
    if fmt == "e4m3":
        byte = np.frexp(amax)[1] - 1 + 127 - 7
    else:
        mant, ex = np.frexp(amax / 6.0)
        byte = np.where(mant > 0.5, ex, ex - 1) + 127
    byte = np.clip(np.where(amax > 0, byte, 1), 1, 254)
    scaled = (w * np.exp2(127.0 - byte)[:, None, :]).reshape(k, n).astype(np.float32)
    by_word = np.ascontiguousarray(scaled.reshape(k // 512, 128, 4, n).transpose(0, 1, 3, 2))
    if fmt == "e4m3":
        words = by_word.astype(ml_dtypes.float8_e4m3fn).view(np.uint8)
    else:
        c = by_word.astype(ml_dtypes.float4_e2m1fn).view(np.uint8) & 0xF
        words = c[..., 0::2] | (c[..., 1::2] << 4)
    return np.ascontiguousarray(words), np.ascontiguousarray(byte.astype(np.uint8).reshape(k // 512, 16, n))


def unpack_weight(words, scales, fmt):
    g, p, n, _ = words.shape
    if fmt == "e4m3":
        vals = np.ascontiguousarray(words).view(ml_dtypes.float8_e4m3fn).astype(np.float64)
    else:
        nib = np.empty((g, p, n, 4), np.uint8)
        nib[..., 0::2] = words & 0xF
        nib[..., 1::2] = words >> 4
        vals = E2M1[nib]
    vals = vals * np.repeat(np.exp2(scales.astype(np.float64) - 127.0), 8, axis=1)[..., None]
    return vals.transpose(0, 1, 3, 2).reshape(g * 512, n)


B, I, H = 512, 1024, 1024
EPS = 1e-12
FORGET_BIAS = 1.0


def layer_norm(x, g, b):
    mean = np.mean(x, axis=-1, keepdims=True)
    var = np.mean((x - mean) ** 2, axis=-1, keepdims=True)
    var_filter = 0.01 * (var < EPS).astype(np.float64)
    normalized = (x - mean) / np.sqrt(var + EPS + var_filter)
    return g * normalized + b


def sigmoid(v):
    return 1.0 / (1.0 + np.exp(-v))


def setup_inputs():
    s, t = mx_kscale(I), mx_kscale(H)
    x = bf(np.random.standard_normal((B, I)) * s)
    hx = bf(np.random.standard_normal((B, H)) * t)
    cx = bf(np.random.standard_normal((B, H)))
    weight_ih = np.random.standard_normal((4 * H, I)) / np.sqrt(I) / s[None, :]
    weight_hh = np.random.standard_normal((4 * H, H)) / np.sqrt(H) / t[None, :]
    gamma = bf(1.0 + 0.1 * np.random.standard_normal((5, H)))
    beta = bf(0.1 * np.random.standard_normal((5, H)))
    ih_words, ih_scales = pack_weight(np.ascontiguousarray(weight_ih.T), "e4m3")
    hh_words, hh_scales = pack_weight(np.ascontiguousarray(weight_hh.T), "e4m3")
    return {"x": x,
            "hx": hx,
            "cx": cx,
            "weight_ih_words": ih_words,
            "weight_ih_scales": ih_scales,
            "weight_hh_words": hh_words,
            "weight_hh_scales": hh_scales,
            "gamma": gamma,
            "beta": beta}


def reference(x, hx, cx, weight_ih_words, weight_ih_scales, weight_hh_words, weight_hh_scales, gamma, beta):
    cx, gamma, beta = f64(cx), f64(gamma), f64(beta)
    gates = (mxq(f64(x), 1, "e4m3") @ unpack_weight(weight_ih_words, weight_ih_scales, "e4m3")) + (mxq(f64(hx), 1, "e4m3") @ unpack_weight(weight_hh_words, weight_hh_scales, "e4m3"))
    ingate, forgetgate, cellgate, outgate = np.split(gates, 4, axis=1)
    ingate = layer_norm(ingate, gamma[0], beta[0])
    forgetgate = layer_norm(forgetgate, gamma[1], beta[1])
    cellgate = layer_norm(cellgate, gamma[2], beta[2])
    outgate = layer_norm(outgate, gamma[3], beta[3])
    ingate = sigmoid(ingate)
    forgetgate = sigmoid(forgetgate + FORGET_BIAS)
    cellgate = np.tanh(cellgate)
    outgate = sigmoid(outgate)
    cy = forgetgate * cx + ingate * cellgate
    cy = layer_norm(cy, gamma[4], beta[4])
    hy = outgate * np.tanh(cy)
    hy_dropped = hy
    return (hy_dropped, hy, cy)

@@ -1,0 +1,340 @@
+from contextlib import ExitStack
+
+import concourse.mybir as mybir
+from concourse.masks import make_identity
+
+F32 = mybir.dt.float32
+BF16 = mybir.dt.bfloat16
+I32 = mybir.dt.int32
+U32 = mybir.dt.uint32
+U8 = mybir.dt.uint8
+FP8X4 = mybir.dt.float8_e4m3fn_x4
+ALU = mybir.AluOpType
+ACT = mybir.ActivationFunctionType
+
+P = 128
+BATCH = 512
+HIDDEN = 1024
+BANK = 512
+K_PASS = 512
+PASSES = 4
+ROW_TILES = BATCH // P
+EPS = 1e-12
+VAR_FILTER = 0.01
+ROOT_HIDDEN = 32.0
+
+GATE_I, GATE_F, GATE_G, GATE_O, NORM_CY = 0, 1, 2, 3, 4
+GATE_ORDER = (GATE_F, GATE_I, GATE_G, GATE_O)
+
+MATMULS_AHEAD = 2
+BETA_AFTER_STATS = 1
+ACT_AFTER_STATS = 2
+HIDDEN_AFTER_G = ACT_AFTER_STATS + 5
+
+PINNED = True
+
+FLOPS = 2 * BATCH * (2 * HIDDEN) * (4 * HIDDEN)
+
+
+def tile_layernormdropoutlstmcell_kernel(
+    tc,
+    x,
+    hx,
+    cx,
+    weight_ih_words,
+    weight_ih_scales,
+    weight_hh_words,
+    weight_hh_scales,
+    gamma,
+    beta,
+    out_0,
+    out_1,
+    out_2,
+):
+    nc = tc.nc
+    with ExitStack() as ctx:
+        const = ctx.enter_context(tc.tile_pool(name="const", bufs=1))
+        stage = ctx.enter_context(tc.tile_pool(name="stage", bufs=2))
+        work = ctx.enter_context(tc.tile_pool(name="work", bufs=3))
+        small = ctx.enter_context(tc.tile_pool(name="small", bufs=6))
+        psum = ctx.enter_context(tc.psum_pool(name="psum", bufs=3))
+        psum_rows = ctx.enter_context(tc.psum_pool(name="psum_rows", bufs=2))
+        if PINNED:
+            ctx.enter_context(tc.manual_schedule())
+
+        one = const.tile([P, 1], F32, name="one")
+        nc.vector.memset(one[:], 1.0)
+        neg_half = const.tile([P, 1], F32, name="neg_half")
+        nc.vector.memset(neg_half[:], -0.5)
+        warm = const.tile([P, 1], F32, name="warm")
+        nc.scalar.activation(out=warm[:], in_=one[:], func=ACT.Sigmoid)
+        ident_f32 = const.tile([P, P], F32, name="ident_f32")
+        make_identity(nc, ident_f32[:])
+        ident_bf16 = const.tile([P, P], BF16, name="ident_bf16")
+        make_identity(nc, ident_bf16[:])
+        ident_x32 = const.tile([P, P], BF16, name="ident_x32")
+
+        xh = [const.tile([P, 2, 2, HIDDEN], BF16, name="xh%d" % pair) for pair in range(2)]
+        for pair in range(2):
+            rows = slice(2 * P * pair, 2 * P * (pair + 1))
+            nc.sync.dma_start(out=xh[pair][:, :, 0, :], in_=x[rows, :].rearrange("(j p) k -> p j k", p=P))
+            nc.sync.dma_start(out=xh[pair][:, :, 1, :], in_=hx[rows, :].rearrange("(j p) k -> p j k", p=P))
+
+        norm_rows = const.tile([P, HIDDEN], BF16, name="norm_rows")
+        nc.vector.memset(norm_rows[:], 0.0)
+        nc.sync.dma_start(out=norm_rows[0:5, :], in_=gamma)
+        nc.sync.dma_start(out=norm_rows[5:10, :], in_=beta)
+
+        w_planes = const.tile([P, 4 * HIDDEN], U8, name="w_planes", align_bytes=64)
+        nc.vector.memset(w_planes[:].bitcast(I32), 0)
+        for w, scales in enumerate((weight_ih_scales, weight_hh_scales)):
+            for quad in range(4):
+                first = 32 * quad + 8 * w
+                nc.sync.dma_start(
+                    out=w_planes[first : first + 8, :].bitcast(I32),
+                    in_=scales[:, 4 * quad : 4 * quad + 4, :].bitcast(I32),
+                )
+
+        w_words = [const.tile([P, 4 * HIDDEN], I32, name="w_words%d" % c, align_bytes=64) for c in range(PASSES)]
+        w_dram = [
+            words[g].rearrange("p n t -> p (n t)").bitcast(I32)
+            for words in (weight_ih_words, weight_hh_words)
+            for g in range(2)
+        ]
+        cx_sb = const.tile([P, ROW_TILES, HIDDEN], BF16, name="cx_sb")
+        for position, gate in enumerate(GATE_ORDER):
+            cols = slice(HIDDEN * gate, HIDDEN * (gate + 1))
+            for c in range(PASSES):
+                nc.sync.dma_start(out=w_words[c][:, cols], in_=w_dram[c][:, cols])
+            if position == 0:
+                nc.sync.dma_start(out=cx_sb[:], in_=cx.rearrange("(m p) k -> p m k", p=P))
+
+        nc.vector.tensor_scalar(out=ident_x32[:], in0=ident_bf16[:], scalar1=ROOT_HIDDEN, scalar2=None, op0=ALU.mult)
+
+        x_codes = [const.tile([P, PASSES * P], U32, name="x_codes%d" % m, align_bytes=64) for m in range(ROW_TILES)]
+        x_planes = [const.tile([P, PASSES * P], U8, name="x_planes%d" % m, align_bytes=64) for m in range(ROW_TILES)]
+        grouped = {}
+
+        def transpose_rows(m):
+            words = xh[m // 2][:, m % 2, :, :].rearrange("p o k -> p (o k)").bitcast(F32)
+            flipped = psum.tile([P, 2 * PASSES, P], F32, tag="acc", name="flipped%d" % m)
+            for c in range(PASSES):
+                for u in range(2):
+                    nc.tensor.transpose(
+                        flipped[:, 2 * c + u, :],
+                        words[:, 256 * c + u : 256 * (c + 1) : 2],
+                        ident_f32[:],
+                    )
+            grouped[m] = stage.tile([P, PASSES * K_PASS], BF16, tag="grouped", name="grouped%d" % m, align_bytes=64)
+            grouped_words = grouped[m][:].bitcast(F32).rearrange("p (c b u) -> p c b u", c=PASSES, u=2)
+            nc.vector.tensor_copy(
+                out=grouped_words[:, 0:2], in_=flipped[:, 0:4, :].rearrange("p (c u) b -> p c b u", u=2)
+            )
+            nc.scalar.copy(
+                out=grouped_words[:, 2:4], in_=flipped[:, 4:8, :].rearrange("p (c u) b -> p c b u", u=2)
+            )
+
+        def quantise_rows(m):
+            nc.vector.quantize_mx(out=x_codes[m][:].bitcast(FP8X4), scales=x_planes[m][:], in_=grouped[m][:])
+
+        gamma_bc = [const.tile([P, HIDDEN], BF16, name="gamma_bc%d" % k) for k in range(5)]
+        beta_bc = [const.tile([P, HIDDEN], BF16, name="beta_bc%d" % k) for k in range(5)]
+        spread = {}
+
+        def spread_norm_rows(k):
+            for row, picker in ((k, ident_x32), (5 + k, ident_bf16)):
+                spread[row] = psum_rows.tile([P, HIDDEN], BF16, tag="spread", name="spread%d" % row)
+                for h in range(2):
+                    cols = slice(BANK * h, BANK * (h + 1))
+                    nc.tensor.matmul(
+                        out=spread[row][:, cols],
+                        lhsT=picker[:, row : row + 1].to_broadcast([P, P]),
+                        rhs=norm_rows[:, cols],
+                        start=True,
+                        stop=True,
+                    )
+
+        def keep_norm_rows(k):
+            nc.vector.tensor_copy(out=gamma_bc[k][:], in_=spread[k][:])
+            nc.scalar.copy(out=beta_bc[k][:], in_=spread[5 + k][:])
+
+        def inverse_std(sum_sq, name):
+            filt = small.tile([P, 1], F32, tag="filt", name="filt_" + name)
+            nc.vector.tensor_scalar(
+                out=filt[:],
+                in0=sum_sq[:],
+                scalar1=EPS * HIDDEN,
+                scalar2=VAR_FILTER * HIDDEN,
+                op0=ALU.is_lt,
+                op1=ALU.mult,
+            )
+            padded = small.tile([P, 1], F32, tag="padded", name="padded_" + name)
+            nc.vector.scalar_tensor_tensor(
+                out=padded[:], in0=filt[:], scalar=EPS * HIDDEN, in1=sum_sq[:], op0=ALU.add, op1=ALU.add
+            )
+            result = small.tile([P, 1], F32, tag="rstd", name="rstd_" + name)
+            nc.gpsimd.tensor_tensor(out=result[:], in0=padded[:], in1=neg_half[:], op=ALU.pow)
+            return result
+
+        acc, neg_mean, sum_sq, rstd, gate_act = {}, {}, {}, {}, {}
+
+        def gate_matmuls(unit):
+            m, gate = unit
+            acc[unit] = psum.tile([P, HIDDEN], F32, tag="acc", name="acc_%d_%d" % unit)
+            for c in range(PASSES):
+                for h in range(2):
+                    cols = slice(HIDDEN * gate + BANK * h, HIDDEN * gate + BANK * (h + 1))
+                    nc.tensor.matmul_mx(
+                        out=acc[unit][:, BANK * h : BANK * (h + 1)],
+                        lhsT=x_codes[m][:, P * c : P * (c + 1)].bitcast(FP8X4),
+                        lhsT_scale=x_planes[m][:, P * c : P * (c + 1)],
+                        rhs=w_words[c][:, cols].bitcast(FP8X4),
+                        rhs_scale=w_planes[4 * c : P, cols],
+                        start=(c == 0),
+                        stop=(c == PASSES - 1),
+                    )
+
+        def gate_stats(unit):
+            name = "%d_%d" % unit
+            raw = work.tile([P, HIDDEN], F32, tag="raw", name="raw_" + name)
+            sums = small.tile([P, 2], F32, tag="sums", name="sums_" + name)
+            for h in range(2):
+                cols = slice(BANK * h, BANK * (h + 1))
+                nc.scalar.activation(
+                    out=raw[:, cols], in_=acc[unit][:, cols], func=ACT.Identity, accum_out=sums[:, h : h + 1]
+                )
+            scaled = small.tile([P, 2], F32, tag="scaled", name="scaled_" + name)
+            neg_mean[unit] = small.tile([P, 1], F32, tag="neg_mean", name="neg_mean_" + name)
+            nc.scalar.activation(
+                out=scaled[:], in_=sums[:], func=ACT.Identity, scale=-1.0 / HIDDEN, accum_out=neg_mean[unit][:]
+            )
+            sum_sq[unit] = small.tile([P, 1], F32, tag="sum_sq", name="sum_sq_" + name)
+            nc.scalar.activation(
+                out=raw[:], in_=raw[:], func=ACT.Square, bias=neg_mean[unit][:], accum_out=sum_sq[unit][:]
+            )
+
+        def gate_times_gamma(unit):
+            gate_act[unit] = const.tile([P, HIDDEN], F32, name="act_%d_%d" % unit)
+            for h in range(2):
+                cols = slice(BANK * h, BANK * (h + 1))
+                nc.vector.scalar_tensor_tensor(
+                    out=gate_act[unit][:, cols],
+                    in0=acc[unit][:, cols],
+                    scalar=neg_mean[unit][:],
+                    in1=gamma_bc[unit[1]][:, cols],
+                    op0=ALU.add,
+                    op1=ALU.mult,
+                )
+
+        def gate_plus_beta(unit):
+            act = gate_act[unit]
+            nc.vector.scalar_tensor_tensor(
+                out=act[:], in0=act[:], scalar=rstd[unit][:], in1=beta_bc[unit[1]][:], op0=ALU.mult, op1=ALU.add
+            )
+
+        def gate_activation(unit):
+            act = gate_act[unit]
+            if unit[1] == GATE_G:
+                nc.scalar.activation(out=act[:], in_=act[:], func=ACT.Tanh)
+            elif unit[1] == GATE_F:
+                nc.scalar.activation(out=act[:], in_=act[:], func=ACT.Sigmoid, bias=one[:])
+            else:
+                nc.scalar.activation(out=act[:], in_=act[:], func=ACT.Sigmoid)
+
+        def forget_times_cx(m):
+            gate_f = gate_act[(m, GATE_F)]
+            nc.vector.tensor_tensor(out=gate_f[:], in0=gate_f[:], in1=cx_sb[:, m, :], op=ALU.mult)
+
+        def cell_sum(m):
+            gate_i, gate_f, gate_g = gate_act[(m, GATE_I)], gate_act[(m, GATE_F)], gate_act[(m, GATE_G)]
+            nc.vector.tensor_tensor(out=gate_i[:], in0=gate_i[:], in1=gate_g[:], op=ALU.mult)
+            total = small.tile([P, 1], F32, tag="total", name="total_%d" % m)
+            nc.vector.scalar_tensor_tensor(
+                out=gate_f[:], in0=gate_f[:], scalar=1.0, in1=gate_i[:], op0=ALU.mult, op1=ALU.add, accum_out=total[:]
+            )
+            neg_mean[m] = small.tile([P, 1], F32, tag="neg_mean_cy", name="neg_mean_cy%d" % m)
+            nc.vector.tensor_scalar(
+                out=neg_mean[m][:], in0=total[:], scalar1=-1.0 / HIDDEN, scalar2=None, op0=ALU.mult
+            )
+            nc.vector.scalar_tensor_tensor(
+                out=gate_i[:], in0=gate_f[:], scalar=neg_mean[m][:], in1=gamma_bc[NORM_CY][:], op0=ALU.add, op1=ALU.mult
+            )
+
+        def cell_squares(m):
+            sum_sq[m] = small.tile([P, 1], F32, tag="sum_sq", name="sum_sq_cy%d" % m)
+            nc.scalar.activation(
+                out=gate_act[(m, GATE_G)][:],
+                in_=gate_act[(m, GATE_F)][:],
+                func=ACT.Square,
+                bias=neg_mean[m][:],
+                accum_out=sum_sq[m][:],
+            )
+            rstd[m] = inverse_std(sum_sq[m], "cy%d" % m)
+
+        def cell_norm(m):
+            cy = gate_act[(m, GATE_I)]
+            nc.vector.scalar_tensor_tensor(
+                out=cy[:], in0=cy[:], scalar=rstd[m][:], in1=beta_bc[NORM_CY][:], op0=ALU.mult, op1=ALU.add
+            )
+            nc.sync.dma_start(out=out_2[P * m : P * (m + 1), :], in_=cy[:])
+
+        def cell_tanh(m):
+            nc.scalar.activation(out=gate_act[(m, GATE_G)][:], in_=gate_act[(m, GATE_I)][:], func=ACT.Tanh)
+
+        def hidden_state(m):
+            gate_o, tanh_cy = gate_act[(m, GATE_O)], gate_act[(m, GATE_G)]
+            nc.vector.tensor_tensor(out=gate_o[:], in0=gate_o[:], in1=tanh_cy[:], op=ALU.mult)
+            nc.sync.dma_start(out=out_0[P * m : P * (m + 1), :], in_=gate_o[:])
+            nc.sync.dma_start(out=out_1[P * m : P * (m + 1), :], in_=gate_o[:])
+
+        units = [(2 * pair + j, gate) for pair in range(2) for gate in GATE_ORDER for j in range(2)]
+        step_of = {}
+        for step, unit in enumerate(units):
+            step_of[unit] = step
+
+        for m in range(ROW_TILES):
+            transpose_rows(m)
+            if m > 0:
+                quantise_rows(m - 1)
+        quantise_rows(ROW_TILES - 1)
+        spread_norm_rows(GATE_ORDER[0])
+        keep_norm_rows(GATE_ORDER[0])
+        for unit in units[:MATMULS_AHEAD]:
+            gate_matmuls(unit)
+
+        for step in range(len(units) + HIDDEN_AFTER_G + 1):
+            new_rows = None
+            if step + MATMULS_AHEAD < len(units):
+                ahead = units[step + MATMULS_AHEAD]
+                if ahead[0] == 0:
+                    new_rows = ahead[1]
+                if ahead == (1, GATE_ORDER[-1]):
+                    new_rows = NORM_CY
+                if new_rows is not None:
+                    spread_norm_rows(new_rows)
+                gate_matmuls(ahead)
+            if step < len(units):
+                gate_stats(units[step])
+                gate_times_gamma(units[step])
+            if 0 <= step - BETA_AFTER_STATS < len(units):
+                gate_plus_beta(units[step - BETA_AFTER_STATS])
+            if step < len(units):
+                rstd[units[step]] = inverse_std(sum_sq[units[step]], "%d_%d" % units[step])
+            if 0 <= step - ACT_AFTER_STATS < len(units):
+                gate_activation(units[step - ACT_AFTER_STATS])
+            if new_rows is not None:
+                keep_norm_rows(new_rows)
+            for m in range(ROW_TILES):
+                if step == step_of[(m, GATE_F)] + ACT_AFTER_STATS + 1:
+                    forget_times_cx(m)
+                since_g = step - step_of[(m, GATE_G)]
+                if since_g == ACT_AFTER_STATS + 1:
+                    cell_sum(m)
+                if since_g == ACT_AFTER_STATS + 2:
+                    cell_squares(m)
+                if since_g == ACT_AFTER_STATS + 3:
+                    cell_norm(m)
+                if since_g == ACT_AFTER_STATS + 4:
+                    cell_tanh(m)
+                if since_g == HIDDEN_AFTER_G:
+                    hidden_state(m)

@@ -27,11 +27,7 @@ GATE_I, GATE_F, GATE_G, GATE_O, NORM_CY = 0, 1, 2, 3, 4
 GATE_ORDER = (GATE_F, GATE_I, GATE_G, GATE_O)
 
 MATMULS_AHEAD = 2
-BETA_AFTER_STATS = 1
-ACT_AFTER_STATS = 2
-HIDDEN_AFTER_G = ACT_AFTER_STATS + 5
-
-PINNED = True
+ACT_AFTER_SUMS = 4
 
 FLOPS = 2 * BATCH * (2 * HIDDEN) * (4 * HIDDEN)
 
@@ -59,8 +55,7 @@ def tile_layernormdropoutlstmcell_kernel(
         small = ctx.enter_context(tc.tile_pool(name="small", bufs=6))
         psum = ctx.enter_context(tc.psum_pool(name="psum", bufs=3))
         psum_rows = ctx.enter_context(tc.psum_pool(name="psum_rows", bufs=2))
-        if PINNED:
-            ctx.enter_context(tc.manual_schedule())
+        ctx.enter_context(tc.manual_schedule())
 
         one = const.tile([P, 1], F32, name="one")
         nc.vector.memset(one[:], 1.0)
@@ -158,25 +153,27 @@ def tile_layernormdropoutlstmcell_kernel(
             nc.vector.tensor_copy(out=gamma_bc[k][:], in_=spread[k][:])
             nc.scalar.copy(out=beta_bc[k][:], in_=spread[5 + k][:])
 
-        def inverse_std(sum_sq, name):
-            filt = small.tile([P, 1], F32, tag="filt", name="filt_" + name)
+        acc, raw, sums, neg_mean, sum_sq, filt, rstd, gate_act = {}, {}, {}, {}, {}, {}, {}, {}
+
+        def variance_filter(key, name):
+            filt[key] = small.tile([P, 1], F32, tag="filt", name="filt_" + name)
             nc.vector.tensor_scalar(
-                out=filt[:],
-                in0=sum_sq[:],
+                out=filt[key][:],
+                in0=sum_sq[key][:],
                 scalar1=EPS * HIDDEN,
                 scalar2=VAR_FILTER * HIDDEN,
                 op0=ALU.is_lt,
                 op1=ALU.mult,
             )
+
+        def inverse_std(key, name):
             padded = small.tile([P, 1], F32, tag="padded", name="padded_" + name)
             nc.vector.scalar_tensor_tensor(
-                out=padded[:], in0=filt[:], scalar=EPS * HIDDEN, in1=sum_sq[:], op0=ALU.add, op1=ALU.add
+                out=padded[:], in0=filt[key][:], scalar=EPS * HIDDEN, in1=sum_sq[key][:], op0=ALU.add, op1=ALU.add
             )
-            result = small.tile([P, 1], F32, tag="rstd", name="rstd_" + name)
-            nc.gpsimd.tensor_tensor(out=result[:], in0=padded[:], in1=neg_half[:], op=ALU.pow)
-            return result
+            rstd[key] = small.tile([P, 1], F32, tag="rstd", name="rstd_" + name)
+            nc.gpsimd.tensor_tensor(out=rstd[key][:], in0=padded[:], in1=neg_half[:], op=ALU.pow)
 
-        acc, neg_mean, sum_sq, rstd, gate_act = {}, {}, {}, {}, {}
 
         def gate_matmuls(unit):
             m, gate = unit
@@ -194,37 +191,49 @@ def tile_layernormdropoutlstmcell_kernel(
                         stop=(c == PASSES - 1),
                     )
 
-        def gate_stats(unit):
+        def gate_sums(unit):
             name = "%d_%d" % unit
-            raw = work.tile([P, HIDDEN], F32, tag="raw", name="raw_" + name)
-            sums = small.tile([P, 2], F32, tag="sums", name="sums_" + name)
+            raw[unit] = work.tile([P, HIDDEN], F32, tag="raw", name="raw_" + name)
+            sums[unit] = small.tile([P, 2], F32, tag="sums", name="sums_" + name)
             for h in range(2):
                 cols = slice(BANK * h, BANK * (h + 1))
                 nc.scalar.activation(
-                    out=raw[:, cols], in_=acc[unit][:, cols], func=ACT.Identity, accum_out=sums[:, h : h + 1]
+                    out=raw[unit][:, cols],
+                    in_=acc[unit][:, cols],
+                    func=ACT.Identity,
+                    accum_out=sums[unit][:, h : h + 1],
                 )
+
+        def gate_mean(unit):
+            name = "%d_%d" % unit
             scaled = small.tile([P, 2], F32, tag="scaled", name="scaled_" + name)
             neg_mean[unit] = small.tile([P, 1], F32, tag="neg_mean", name="neg_mean_" + name)
             nc.scalar.activation(
-                out=scaled[:], in_=sums[:], func=ACT.Identity, scale=-1.0 / HIDDEN, accum_out=neg_mean[unit][:]
-            )
-            sum_sq[unit] = small.tile([P, 1], F32, tag="sum_sq", name="sum_sq_" + name)
-            nc.scalar.activation(
-                out=raw[:], in_=raw[:], func=ACT.Square, bias=neg_mean[unit][:], accum_out=sum_sq[unit][:]
+                out=scaled[:], in_=sums[unit][:], func=ACT.Identity, scale=-1.0 / HIDDEN, accum_out=neg_mean[unit][:]
             )
 
-        def gate_times_gamma(unit):
-            gate_act[unit] = const.tile([P, HIDDEN], F32, name="act_%d_%d" % unit)
-            for h in range(2):
-                cols = slice(BANK * h, BANK * (h + 1))
-                nc.vector.scalar_tensor_tensor(
-                    out=gate_act[unit][:, cols],
-                    in0=acc[unit][:, cols],
-                    scalar=neg_mean[unit][:],
-                    in1=gamma_bc[unit[1]][:, cols],
-                    op0=ALU.add,
-                    op1=ALU.mult,
-                )
+        def gate_squares(unit):
+            sum_sq[unit] = small.tile([P, 1], F32, tag="sum_sq", name="sum_sq_%d_%d" % unit)
+            nc.scalar.activation(
+                out=raw[unit][:],
+                in_=raw[unit][:],
+                func=ACT.Square,
+                bias=neg_mean[unit][:],
+                accum_out=sum_sq[unit][:],
+            )
+
+        def gate_times_gamma(unit, h):
+            if h == 0:
+                gate_act[unit] = const.tile([P, HIDDEN], F32, name="act_%d_%d" % unit)
+            cols = slice(BANK * h, BANK * (h + 1))
+            nc.vector.scalar_tensor_tensor(
+                out=gate_act[unit][:, cols],
+                in0=acc[unit][:, cols],
+                scalar=neg_mean[unit][:],
+                in1=gamma_bc[unit[1]][:, cols],
+                op0=ALU.add,
+                op1=ALU.mult,
+            )
 
         def gate_plus_beta(unit):
             act = gate_act[unit]
@@ -245,19 +254,30 @@ def tile_layernormdropoutlstmcell_kernel(
             gate_f = gate_act[(m, GATE_F)]
             nc.vector.tensor_tensor(out=gate_f[:], in0=gate_f[:], in1=cx_sb[:, m, :], op=ALU.mult)
 
+        total = {}
+
         def cell_sum(m):
             gate_i, gate_f, gate_g = gate_act[(m, GATE_I)], gate_act[(m, GATE_F)], gate_act[(m, GATE_G)]
             nc.vector.tensor_tensor(out=gate_i[:], in0=gate_i[:], in1=gate_g[:], op=ALU.mult)
-            total = small.tile([P, 1], F32, tag="total", name="total_%d" % m)
+            total[m] = small.tile([P, 1], F32, tag="total", name="total_%d" % m)
             nc.vector.scalar_tensor_tensor(
-                out=gate_f[:], in0=gate_f[:], scalar=1.0, in1=gate_i[:], op0=ALU.mult, op1=ALU.add, accum_out=total[:]
+                out=gate_f[:], in0=gate_f[:], scalar=1.0, in1=gate_i[:], op0=ALU.mult, op1=ALU.add, accum_out=total[m][:]
             )
+
+        def cell_mean(m):
             neg_mean[m] = small.tile([P, 1], F32, tag="neg_mean_cy", name="neg_mean_cy%d" % m)
             nc.vector.tensor_scalar(
-                out=neg_mean[m][:], in0=total[:], scalar1=-1.0 / HIDDEN, scalar2=None, op0=ALU.mult
+                out=neg_mean[m][:], in0=total[m][:], scalar1=-1.0 / HIDDEN, scalar2=None, op0=ALU.mult
             )
+
+        def cell_times_gamma(m):
             nc.vector.scalar_tensor_tensor(
-                out=gate_i[:], in0=gate_f[:], scalar=neg_mean[m][:], in1=gamma_bc[NORM_CY][:], op0=ALU.add, op1=ALU.mult
+                out=gate_act[(m, GATE_I)][:],
+                in0=gate_act[(m, GATE_F)][:],
+                scalar=neg_mean[m][:],
+                in1=gamma_bc[NORM_CY][:],
+                op0=ALU.add,
+                op1=ALU.mult,
             )
 
         def cell_squares(m):
@@ -269,7 +289,6 @@ def tile_layernormdropoutlstmcell_kernel(
                 bias=neg_mean[m][:],
                 accum_out=sum_sq[m][:],
             )
-            rstd[m] = inverse_std(sum_sq[m], "cy%d" % m)
 
         def cell_norm(m):
             cy = gate_act[(m, GATE_I)]
@@ -302,39 +321,66 @@ def tile_layernormdropoutlstmcell_kernel(
         for unit in units[:MATMULS_AHEAD]:
             gate_matmuls(unit)
 
-        for step in range(len(units) + HIDDEN_AFTER_G + 1):
-            new_rows = None
-            if step + MATMULS_AHEAD < len(units):
-                ahead = units[step + MATMULS_AHEAD]
-                if ahead[0] == 0:
-                    new_rows = ahead[1]
-                if ahead == (1, GATE_ORDER[-1]):
-                    new_rows = NORM_CY
-                if new_rows is not None:
-                    spread_norm_rows(new_rows)
-                gate_matmuls(ahead)
-            if step < len(units):
-                gate_stats(units[step])
-                gate_times_gamma(units[step])
-            if 0 <= step - BETA_AFTER_STATS < len(units):
-                gate_plus_beta(units[step - BETA_AFTER_STATS])
-            if step < len(units):
-                rstd[units[step]] = inverse_std(sum_sq[units[step]], "%d_%d" % units[step])
-            if 0 <= step - ACT_AFTER_STATS < len(units):
-                gate_activation(units[step - ACT_AFTER_STATS])
-            if new_rows is not None:
-                keep_norm_rows(new_rows)
+        def unit_at(step):
+            return units[step] if 0 <= step < len(units) else None
+
+        spread_rows = None
+        for step in range(len(units) + ACT_AFTER_SUMS + 7):
+            due = {}
             for m in range(ROW_TILES):
-                if step == step_of[(m, GATE_F)] + ACT_AFTER_STATS + 1:
+                due[step - step_of[(m, GATE_G)] - ACT_AFTER_SUMS] = m
+
+            if unit_at(step - 2):
+                variance_filter(unit_at(step - 2), "%d_%d" % unit_at(step - 2))
+            if 2 in due:
+                cell_mean(due[2])
+            if 3 in due:
+                variance_filter(due[3], "cy%d" % due[3])
+
+            if unit_at(step):
+                gate_sums(unit_at(step))
+            if unit_at(step - 1):
+                gate_squares(unit_at(step - 1))
+            if unit_at(step):
+                gate_mean(unit_at(step))
+            if unit_at(step - ACT_AFTER_SUMS):
+                gate_activation(unit_at(step - ACT_AFTER_SUMS))
+            if 2 in due:
+                cell_squares(due[2])
+            if 5 in due:
+                cell_tanh(due[5])
+
+            if unit_at(step - 1):
+                gate_times_gamma(unit_at(step - 1), 0)
+            if unit_at(step - 2):
+                inverse_std(unit_at(step - 2), "%d_%d" % unit_at(step - 2))
+            if 3 in due:
+                inverse_std(due[3], "cy%d" % due[3])
+            if unit_at(step - 1):
+                gate_times_gamma(unit_at(step - 1), 1)
+            if unit_at(step - 3):
+                gate_plus_beta(unit_at(step - 3))
+            for m in range(ROW_TILES):
+                if step == step_of[(m, GATE_F)] + ACT_AFTER_SUMS + 1:
                     forget_times_cx(m)
-                since_g = step - step_of[(m, GATE_G)]
-                if since_g == ACT_AFTER_STATS + 1:
-                    cell_sum(m)
-                if since_g == ACT_AFTER_STATS + 2:
-                    cell_squares(m)
-                if since_g == ACT_AFTER_STATS + 3:
-                    cell_norm(m)
-                if since_g == ACT_AFTER_STATS + 4:
-                    cell_tanh(m)
-                if since_g == HIDDEN_AFTER_G:
-                    hidden_state(m)
+            if 1 in due:
+                cell_sum(due[1])
+            if 2 in due:
+                cell_times_gamma(due[2])
+            if 4 in due:
+                cell_norm(due[4])
+            if 6 in due:
+                hidden_state(due[6])
+
+            if spread_rows is not None:
+                keep_norm_rows(spread_rows)
+                spread_rows = None
+            ahead = unit_at(step + MATMULS_AHEAD)
+            if ahead:
+                if ahead[0] == 0:
+                    spread_rows = ahead[1]
+                if ahead == (1, GATE_ORDER[-1]):
+                    spread_rows = NORM_CY
+                if spread_rows is not None:
+                    spread_norm_rows(spread_rows)
+                gate_matmuls(ahead)

@@ -25,8 +25,10 @@ ROOT_HIDDEN = 32.0
 
 GATE_I, GATE_F, GATE_G, GATE_O, NORM_CY = 0, 1, 2, 3, 4
 GATE_ORDER = (GATE_F, GATE_I, GATE_G, GATE_O)
+TURNED = (GATE_I, GATE_G)
+COLUMN_TILES = HIDDEN // P
 
-MATMULS_AHEAD = 2
+MATMULS_AHEAD = 1
 ACT_AFTER_SUMS = 4
 
 FLOPS = 2 * BATCH * (2 * HIDDEN) * (4 * HIDDEN)
@@ -52,9 +54,8 @@ def tile_layernormdropoutlstmcell_kernel(
         const = ctx.enter_context(tc.tile_pool(name="const", bufs=1))
         stage = ctx.enter_context(tc.tile_pool(name="stage", bufs=2))
         work = ctx.enter_context(tc.tile_pool(name="work", bufs=3))
-        small = ctx.enter_context(tc.tile_pool(name="small", bufs=6))
-        psum = ctx.enter_context(tc.psum_pool(name="psum", bufs=3))
-        psum_rows = ctx.enter_context(tc.psum_pool(name="psum_rows", bufs=2))
+        small = ctx.enter_context(tc.tile_pool(name="small", bufs=8))
+        psum = ctx.enter_context(tc.psum_pool(name="psum", bufs=4))
         ctx.enter_context(tc.manual_schedule())
 
         one = const.tile([P, 1], F32, name="one")
@@ -70,10 +71,13 @@ def tile_layernormdropoutlstmcell_kernel(
         ident_x32 = const.tile([P, P], BF16, name="ident_x32")
 
         xh = [const.tile([P, 2, 2, HIDDEN], BF16, name="xh%d" % pair) for pair in range(2)]
-        for pair in range(2):
+
+        def load_rows(pair):
             rows = slice(2 * P * pair, 2 * P * (pair + 1))
             nc.sync.dma_start(out=xh[pair][:, :, 0, :], in_=x[rows, :].rearrange("(j p) k -> p j k", p=P))
             nc.sync.dma_start(out=xh[pair][:, :, 1, :], in_=hx[rows, :].rearrange("(j p) k -> p j k", p=P))
+
+        load_rows(0)
 
         norm_rows = const.tile([P, HIDDEN], BF16, name="norm_rows")
         nc.vector.memset(norm_rows[:], 0.0)
@@ -96,53 +100,63 @@ def tile_layernormdropoutlstmcell_kernel(
             for words in (weight_ih_words, weight_hh_words)
             for g in range(2)
         ]
-        cx_sb = const.tile([P, ROW_TILES, HIDDEN], BF16, name="cx_sb")
-        for position, gate in enumerate(GATE_ORDER):
+
+        def load_gate(gate):
             cols = slice(HIDDEN * gate, HIDDEN * (gate + 1))
             for c in range(PASSES):
                 nc.sync.dma_start(out=w_words[c][:, cols], in_=w_dram[c][:, cols])
-            if position == 0:
-                nc.sync.dma_start(out=cx_sb[:], in_=cx.rearrange("(m p) k -> p m k", p=P))
+
+        cx_sb = const.tile([P, ROW_TILES, HIDDEN], BF16, name="cx_sb")
+        load_gate(GATE_F)
+        load_gate(GATE_I)
+        load_rows(1)
+        load_gate(GATE_G)
+        nc.sync.dma_start(out=cx_sb[:], in_=cx.rearrange("(m p) k -> p m k", p=P))
+        load_gate(GATE_O)
 
         nc.vector.tensor_scalar(out=ident_x32[:], in0=ident_bf16[:], scalar1=ROOT_HIDDEN, scalar2=None, op0=ALU.mult)
 
         x_codes = [const.tile([P, PASSES * P], U32, name="x_codes%d" % m, align_bytes=64) for m in range(ROW_TILES)]
         x_planes = [const.tile([P, PASSES * P], U8, name="x_planes%d" % m, align_bytes=64) for m in range(ROW_TILES)]
-        grouped = {}
+        grouped, flipped = {}, {}
 
         def transpose_rows(m):
             words = xh[m // 2][:, m % 2, :, :].rearrange("p o k -> p (o k)").bitcast(F32)
-            flipped = psum.tile([P, 2 * PASSES, P], F32, tag="acc", name="flipped%d" % m)
+            flipped[m] = psum.tile([P, 2 * PASSES, P], F32, tag="slot", name="flipped%d" % m)
             for c in range(PASSES):
                 for u in range(2):
                     nc.tensor.transpose(
-                        flipped[:, 2 * c + u, :],
+                        flipped[m][:, 2 * c + u, :],
                         words[:, 256 * c + u : 256 * (c + 1) : 2],
                         ident_f32[:],
                     )
-            grouped[m] = stage.tile([P, PASSES * K_PASS], BF16, tag="grouped", name="grouped%d" % m, align_bytes=64)
+
+        def keep_rows(m, bank):
+            if bank == 0:
+                grouped[m] = stage.tile([P, PASSES * K_PASS], BF16, tag="grouped", name="grouped%d" % m, align_bytes=64)
             grouped_words = grouped[m][:].bitcast(F32).rearrange("p (c b u) -> p c b u", c=PASSES, u=2)
-            nc.vector.tensor_copy(
-                out=grouped_words[:, 0:2], in_=flipped[:, 0:4, :].rearrange("p (c u) b -> p c b u", u=2)
-            )
-            nc.scalar.copy(
-                out=grouped_words[:, 2:4], in_=flipped[:, 4:8, :].rearrange("p (c u) b -> p c b u", u=2)
-            )
+            turned_words = flipped[m][:, 4 * bank : 4 * bank + 4, :].rearrange("p (c u) b -> p c b u", u=2)
+            if bank == 0:
+                nc.vector.tensor_copy(out=grouped_words[:, 0:2], in_=turned_words)
+            else:
+                nc.scalar.copy(out=grouped_words[:, 2:4], in_=turned_words)
 
         def quantise_rows(m):
             nc.vector.quantize_mx(out=x_codes[m][:].bitcast(FP8X4), scales=x_planes[m][:], in_=grouped[m][:])
 
-        gamma_bc = [const.tile([P, HIDDEN], BF16, name="gamma_bc%d" % k) for k in range(5)]
-        beta_bc = [const.tile([P, HIDDEN], BF16, name="beta_bc%d" % k) for k in range(5)]
+        gamma_bc, beta_bc = {}, {}
+        for k in (GATE_F, GATE_O, NORM_CY):
+            gamma_bc[k] = const.tile([P, HIDDEN], BF16, name="gamma_bc%d" % k)
+            beta_bc[k] = const.tile([P, HIDDEN], BF16, name="beta_bc%d" % k)
         spread = {}
 
         def spread_norm_rows(k):
-            for row, picker in ((k, ident_x32), (5 + k, ident_bf16)):
-                spread[row] = psum_rows.tile([P, HIDDEN], BF16, tag="spread", name="spread%d" % row)
+            spread[k] = psum.tile([P, 2, HIDDEN], BF16, tag="slot", name="spread%d" % k)
+            for which, row, picker in ((0, k, ident_x32), (1, 5 + k, ident_bf16)):
                 for h in range(2):
                     cols = slice(BANK * h, BANK * (h + 1))
                     nc.tensor.matmul(
-                        out=spread[row][:, cols],
+                        out=spread[k][:, which, cols],
                         lhsT=picker[:, row : row + 1].to_broadcast([P, P]),
                         rhs=norm_rows[:, cols],
                         start=True,
@@ -150,8 +164,16 @@ def tile_layernormdropoutlstmcell_kernel(
                     )
 
         def keep_norm_rows(k):
-            nc.vector.tensor_copy(out=gamma_bc[k][:], in_=spread[k][:])
-            nc.scalar.copy(out=beta_bc[k][:], in_=spread[5 + k][:])
+            nc.vector.tensor_copy(out=gamma_bc[k][:], in_=spread[k][:, 0, :])
+            nc.vector.tensor_copy(out=beta_bc[k][:], in_=spread[k][:, 1, :])
+
+        norm_cols = const.tile([P, COLUMN_TILES, 10], F32, name="norm_cols")
+
+        def turn_norm_rows():
+            turned_rows = psum.tile([P, COLUMN_TILES, P], BF16, tag="slot", name="turned_rows")
+            for j in range(COLUMN_TILES):
+                nc.tensor.transpose(turned_rows[:, j, :], norm_rows[:, P * j : P * (j + 1)], ident_bf16[:])
+            nc.vector.tensor_copy(out=norm_cols[:], in_=turned_rows[:, :, 0:10])
 
         acc, raw, sums, neg_mean, sum_sq, filt, rstd, gate_act = {}, {}, {}, {}, {}, {}, {}, {}
 
@@ -177,7 +199,7 @@ def tile_layernormdropoutlstmcell_kernel(
 
         def gate_matmuls(unit):
             m, gate = unit
-            acc[unit] = psum.tile([P, HIDDEN], F32, tag="acc", name="acc_%d_%d" % unit)
+            acc[unit] = psum.tile([P, HIDDEN], F32, tag="slot", name="acc_%d_%d" % unit)
             for c in range(PASSES):
                 for h in range(2):
                     cols = slice(HIDDEN * gate + BANK * h, HIDDEN * gate + BANK * (h + 1))
@@ -250,24 +272,115 @@ def tile_layernormdropoutlstmcell_kernel(
             else:
                 nc.scalar.activation(out=act[:], in_=act[:], func=ACT.Sigmoid)
 
+        stats, mean_var, bias, normal, turned = {}, {}, {}, {}, {}
+
+        def turned_stats(unit):
+            stats[unit] = small.tile([P, 2, 6], F32, tag="stats", name="stats_%d_%d" % unit)
+            for h in range(2):
+                nc.vector.bn_stats(out=stats[unit][:, h, :], in_=acc[unit][:, BANK * h : BANK * (h + 1)])
+
+        def turned_aggregate(unit):
+            mean_var[unit] = small.tile([P, 2], F32, tag="mean_var", name="mean_var_%d_%d" % unit)
+            nc.vector.bn_aggr(out=mean_var[unit][:], in_=stats[unit][:].rearrange("p h s -> p (h s)"))
+
+        def turned_filter(unit):
+            filt[unit] = small.tile([P, 1], F32, tag="filt", name="filt_%d_%d" % unit)
+            nc.vector.tensor_scalar(
+                out=filt[unit][:],
+                in0=mean_var[unit][:, 1:2],
+                scalar1=EPS,
+                scalar2=VAR_FILTER,
+                op0=ALU.is_lt,
+                op1=ALU.mult,
+            )
+
+        def turned_inverse_std(unit):
+            padded = small.tile([P, 1], F32, tag="padded", name="padded_%d_%d" % unit)
+            nc.vector.scalar_tensor_tensor(
+                out=padded[:], in0=filt[unit][:], scalar=EPS, in1=mean_var[unit][:, 1:2], op0=ALU.add, op1=ALU.add
+            )
+            rstd[unit] = small.tile([P, 1], F32, tag="rstd", name="rstd_%d_%d" % unit)
+            nc.gpsimd.tensor_tensor(out=rstd[unit][:], in0=padded[:], in1=neg_half[:], op=ALU.pow)
+
+        def turned_bias(unit):
+            bias[unit] = small.tile([P, 1], F32, tag="bias", name="bias_%d_%d" % unit)
+            nc.vector.scalar_tensor_tensor(
+                out=bias[unit][:], in0=mean_var[unit][:, 0:1], scalar=-1.0, in1=rstd[unit][:], op0=ALU.mult, op1=ALU.mult
+            )
+
+        def turned_normalise(unit):
+            normal[unit] = work.tile([P, HIDDEN], F32, tag="normal", name="normal_%d_%d" % unit)
+            for h in range(2):
+                cols = slice(BANK * h, BANK * (h + 1))
+                nc.scalar.activation(
+                    out=normal[unit][:, cols],
+                    in_=acc[unit][:, cols],
+                    func=ACT.Identity,
+                    scale=rstd[unit][:],
+                    bias=bias[unit][:],
+                )
+
+        def turned_transpose(unit):
+            turned[unit] = psum.tile([P, HIDDEN], F32, tag="slot", name="turned_%d_%d" % unit)
+            for j in range(COLUMN_TILES):
+                cols = slice(P * j, P * (j + 1))
+                nc.tensor.transpose(turned[unit][:, cols], normal[unit][:, cols], ident_f32[:])
+
+        def turned_activation(unit):
+            gate = unit[1]
+            gate_act[unit] = const.tile([P, HIDDEN], F32, name="act_%d_%d" % unit)
+            for j in range(COLUMN_TILES):
+                cols = slice(P * j, P * (j + 1))
+                nc.scalar.activation(
+                    out=gate_act[unit][:, cols],
+                    in_=turned[unit][:, cols],
+                    func=ACT.Tanh if gate == GATE_G else ACT.Sigmoid,
+                    scale=norm_cols[:, j, gate : gate + 1],
+                    bias=norm_cols[:, j, 5 + gate : 6 + gate],
+                )
+
         def forget_times_cx(m):
             gate_f = gate_act[(m, GATE_F)]
             nc.vector.tensor_tensor(out=gate_f[:], in0=gate_f[:], in1=cx_sb[:, m, :], op=ALU.mult)
 
-        total = {}
+        total, product = {}, {}
 
-        def cell_sum(m):
-            gate_i, gate_f, gate_g = gate_act[(m, GATE_I)], gate_act[(m, GATE_F)], gate_act[(m, GATE_G)]
+        def cell_product(m):
+            gate_i, gate_g = gate_act[(m, GATE_I)], gate_act[(m, GATE_G)]
             nc.vector.tensor_tensor(out=gate_i[:], in0=gate_i[:], in1=gate_g[:], op=ALU.mult)
-            total[m] = small.tile([P, 1], F32, tag="total", name="total_%d" % m)
+
+        def cell_product_back(m):
+            product[m] = psum.tile([P, HIDDEN], F32, tag="slot", name="product%d" % m)
+            for j in range(COLUMN_TILES):
+                cols = slice(P * j, P * (j + 1))
+                nc.tensor.transpose(product[m][:, cols], gate_act[(m, GATE_I)][:, cols], ident_f32[:])
+
+        def cell_sum(m, h):
+            if h == 0:
+                total[m] = small.tile([P, 2], F32, tag="total", name="total_%d" % m)
+            gate_f = gate_act[(m, GATE_F)]
+            cols = slice(BANK * h, BANK * (h + 1))
             nc.vector.scalar_tensor_tensor(
-                out=gate_f[:], in0=gate_f[:], scalar=1.0, in1=gate_i[:], op0=ALU.mult, op1=ALU.add, accum_out=total[m][:]
+                out=gate_f[:, cols],
+                in0=gate_f[:, cols],
+                scalar=1.0,
+                in1=product[m][:, cols],
+                op0=ALU.mult,
+                op1=ALU.add,
+                accum_out=total[m][:, h : h + 1],
             )
 
         def cell_mean(m):
+            scaled = small.tile([P, 2], F32, tag="scaled_cy", name="scaled_cy%d" % m)
             neg_mean[m] = small.tile([P, 1], F32, tag="neg_mean_cy", name="neg_mean_cy%d" % m)
             nc.vector.tensor_scalar(
-                out=neg_mean[m][:], in0=total[m][:], scalar1=-1.0 / HIDDEN, scalar2=None, op0=ALU.mult
+                out=scaled[:],
+                in0=total[m][:],
+                scalar1=-1.0 / HIDDEN,
+                scalar2=None,
+                op0=ALU.mult,
+                op1=ALU.add,
+                accum_out=neg_mean[m][:],
             )
 
         def cell_times_gamma(m):
@@ -306,81 +419,126 @@ def tile_layernormdropoutlstmcell_kernel(
             nc.sync.dma_start(out=out_0[P * m : P * (m + 1), :], in_=gate_o[:])
             nc.sync.dma_start(out=out_1[P * m : P * (m + 1), :], in_=gate_o[:])
 
-        units = [(2 * pair + j, gate) for pair in range(2) for gate in GATE_ORDER for j in range(2)]
+        units = [(m, gate) for gate in (GATE_F, GATE_I, GATE_G) for m in (0, 1)]
+        units += [(m, gate) for m in (2, 3) for gate in (GATE_F, GATE_I, GATE_G)]
+        units += [(m, GATE_O) for m in range(ROW_TILES)]
         step_of = {}
         for step, unit in enumerate(units):
             step_of[unit] = step
 
-        for m in range(ROW_TILES):
+        for m in (0, 1):
             transpose_rows(m)
-            if m > 0:
-                quantise_rows(m - 1)
-        quantise_rows(ROW_TILES - 1)
-        spread_norm_rows(GATE_ORDER[0])
-        keep_norm_rows(GATE_ORDER[0])
+            keep_rows(m, 0)
+            keep_rows(m, 1)
+        quantise_rows(0)
+        quantise_rows(1)
+        turn_norm_rows()
+        spread_norm_rows(GATE_F)
+        keep_norm_rows(GATE_F)
         for unit in units[:MATMULS_AHEAD]:
             gate_matmuls(unit)
 
-        def unit_at(step):
-            return units[step] if 0 <= step < len(units) else None
+        def plain_at(step):
+            unit = units[step] if 0 <= step < len(units) else None
+            return unit if unit and unit[1] not in TURNED else None
 
-        spread_rows = None
-        for step in range(len(units) + ACT_AFTER_SUMS + 7):
+        def turned_at(step):
+            unit = units[step] if 0 <= step < len(units) else None
+            return unit if unit and unit[1] in TURNED else None
+
+        early_rows = {6: NORM_CY, 10: GATE_O}
+        late_rows = {2: 2, 3: 3}
+
+        PRODUCT_AFTER_STATS = 3
+        hidden_step = {}
+        for m in range(ROW_TILES):
+            hidden_step[m] = max(
+                step_of[(m, GATE_G)] + PRODUCT_AFTER_STATS + 6, step_of[(m, GATE_O)] + ACT_AFTER_SUMS + 1
+            )
+
+        for step in range(max([hidden_step[m] for m in range(ROW_TILES)]) + 1):
             due = {}
             for m in range(ROW_TILES):
-                due[step - step_of[(m, GATE_G)] - ACT_AFTER_SUMS] = m
+                due[step - step_of[(m, GATE_G)] - PRODUCT_AFTER_STATS] = m
 
-            if unit_at(step - 2):
-                variance_filter(unit_at(step - 2), "%d_%d" % unit_at(step - 2))
+            if plain_at(step - 2):
+                variance_filter(plain_at(step - 2), "%d_%d" % plain_at(step - 2))
             if 2 in due:
                 cell_mean(due[2])
             if 3 in due:
                 variance_filter(due[3], "cy%d" % due[3])
 
-            if unit_at(step):
-                gate_sums(unit_at(step))
-            if unit_at(step - 1):
-                gate_squares(unit_at(step - 1))
-            if unit_at(step):
-                gate_mean(unit_at(step))
-            if unit_at(step - ACT_AFTER_SUMS):
-                gate_activation(unit_at(step - ACT_AFTER_SUMS))
+            longs, smalls = [], []
+            if turned_at(step):
+                turned_stats(turned_at(step))
+            if turned_at(step - 1):
+                turned_bias(turned_at(step - 1))
+            if turned_at(step):
+                smalls.append((turned_aggregate, (turned_at(step),)))
+                smalls.append((turned_filter, (turned_at(step),)))
+                smalls.append((turned_inverse_std, (turned_at(step),)))
+            if plain_at(step - 2):
+                smalls.append((inverse_std, (plain_at(step - 2), "%d_%d" % plain_at(step - 2))))
+            if 3 in due:
+                smalls.append((inverse_std, (due[3], "cy%d" % due[3])))
+            if plain_at(step - 1):
+                longs.append((gate_times_gamma, (plain_at(step - 1), 0)))
+                longs.append((gate_times_gamma, (plain_at(step - 1), 1)))
+            if 1 in due:
+                longs.append((cell_sum, (due[1], 0)))
+                longs.append((cell_sum, (due[1], 1)))
+            if plain_at(step - 3):
+                longs.append((gate_plus_beta, (plain_at(step - 3),)))
+            for m in range(ROW_TILES):
+                if step == step_of[(m, GATE_F)] + ACT_AFTER_SUMS + 1:
+                    longs.append((forget_times_cx, (m,)))
+            if 0 in due:
+                longs.append((cell_product, (due[0],)))
+            if 2 in due:
+                longs.append((cell_times_gamma, (due[2],)))
+            if 4 in due:
+                longs.append((cell_norm, (due[4],)))
+            for m in range(ROW_TILES):
+                if step == hidden_step[m]:
+                    longs.append((hidden_state, (m,)))
+            if step - 1 in early_rows:
+                longs.append((keep_norm_rows, (early_rows[step - 1],)))
+            if step - 1 in late_rows:
+                longs.append((keep_rows, (late_rows[step - 1], 0)))
+            if step - 2 in late_rows:
+                longs.append((quantise_rows, (late_rows[step - 2],)))
+            for position in range(max(len(longs), len(smalls))):
+                if position < len(longs):
+                    longs[position][0](*longs[position][1])
+                if position < len(smalls):
+                    smalls[position][0](*smalls[position][1])
+
+            if plain_at(step):
+                gate_sums(plain_at(step))
+            if turned_at(step - 1):
+                turned_normalise(turned_at(step - 1))
+            if plain_at(step - 1):
+                gate_squares(plain_at(step - 1))
+            if plain_at(step):
+                gate_mean(plain_at(step))
+            if turned_at(step - 2):
+                turned_activation(turned_at(step - 2))
+            if plain_at(step - ACT_AFTER_SUMS):
+                gate_activation(plain_at(step - ACT_AFTER_SUMS))
             if 2 in due:
                 cell_squares(due[2])
             if 5 in due:
                 cell_tanh(due[5])
+            if step - 1 in late_rows:
+                keep_rows(late_rows[step - 1], 1)
 
-            if unit_at(step - 1):
-                gate_times_gamma(unit_at(step - 1), 0)
-            if unit_at(step - 2):
-                inverse_std(unit_at(step - 2), "%d_%d" % unit_at(step - 2))
-            if 3 in due:
-                inverse_std(due[3], "cy%d" % due[3])
-            if unit_at(step - 1):
-                gate_times_gamma(unit_at(step - 1), 1)
-            if unit_at(step - 3):
-                gate_plus_beta(unit_at(step - 3))
-            for m in range(ROW_TILES):
-                if step == step_of[(m, GATE_F)] + ACT_AFTER_SUMS + 1:
-                    forget_times_cx(m)
-            if 1 in due:
-                cell_sum(due[1])
-            if 2 in due:
-                cell_times_gamma(due[2])
-            if 4 in due:
-                cell_norm(due[4])
-            if 6 in due:
-                hidden_state(due[6])
-
-            if spread_rows is not None:
-                keep_norm_rows(spread_rows)
-                spread_rows = None
-            ahead = unit_at(step + MATMULS_AHEAD)
-            if ahead:
-                if ahead[0] == 0:
-                    spread_rows = ahead[1]
-                if ahead == (1, GATE_ORDER[-1]):
-                    spread_rows = NORM_CY
-                if spread_rows is not None:
-                    spread_norm_rows(spread_rows)
-                gate_matmuls(ahead)
+            if 0 <= step + MATMULS_AHEAD < len(units):
+                gate_matmuls(units[step + MATMULS_AHEAD])
+            if turned_at(step - 1):
+                turned_transpose(turned_at(step - 1))
+            if 0 in due:
+                cell_product_back(due[0])
+            if step in early_rows:
+                spread_norm_rows(early_rows[step])
+            if step in late_rows:
+                transpose_rows(late_rows[step])

@@ -25,7 +25,7 @@ ROOT_HIDDEN = 32.0
 
 GATE_I, GATE_F, GATE_G, GATE_O, NORM_CY = 0, 1, 2, 3, 4
 GATE_ORDER = (GATE_F, GATE_I, GATE_G, GATE_O)
-TURNED = (GATE_I, GATE_G)
+TURNED = (GATE_I, GATE_G, GATE_O)
 COLUMN_TILES = HIDDEN // P
 
 MATMULS_AHEAD = 1
@@ -145,7 +145,7 @@ def tile_layernormdropoutlstmcell_kernel(
             nc.vector.quantize_mx(out=x_codes[m][:].bitcast(FP8X4), scales=x_planes[m][:], in_=grouped[m][:])
 
         gamma_bc, beta_bc = {}, {}
-        for k in (GATE_F, GATE_O, NORM_CY):
+        for k in (GATE_F, NORM_CY):
             gamma_bc[k] = const.tile([P, HIDDEN], BF16, name="gamma_bc%d" % k)
             beta_bc[k] = const.tile([P, HIDDEN], BF16, name="beta_bc%d" % k)
         spread = {}
@@ -413,11 +413,21 @@ def tile_layernormdropoutlstmcell_kernel(
         def cell_tanh(m):
             nc.scalar.activation(out=gate_act[(m, GATE_G)][:], in_=gate_act[(m, GATE_I)][:], func=ACT.Tanh)
 
+        out_gate = {}
+
+        def out_gate_back(m):
+            out_gate[m] = psum.tile([P, HIDDEN], F32, tag="slot", name="out_gate%d" % m)
+            for j in range(COLUMN_TILES):
+                cols = slice(P * j, P * (j + 1))
+                nc.tensor.transpose(out_gate[m][:, cols], gate_act[(m, GATE_O)][:, cols], ident_f32[:])
+
         def hidden_state(m):
-            gate_o, tanh_cy = gate_act[(m, GATE_O)], gate_act[(m, GATE_G)]
-            nc.vector.tensor_tensor(out=gate_o[:], in0=gate_o[:], in1=tanh_cy[:], op=ALU.mult)
-            nc.sync.dma_start(out=out_0[P * m : P * (m + 1), :], in_=gate_o[:])
-            nc.sync.dma_start(out=out_1[P * m : P * (m + 1), :], in_=gate_o[:])
+            tanh_cy = gate_act[(m, GATE_G)]
+            for h in range(2):
+                cols = slice(BANK * h, BANK * (h + 1))
+                nc.vector.tensor_tensor(out=tanh_cy[:, cols], in0=tanh_cy[:, cols], in1=out_gate[m][:, cols], op=ALU.mult)
+            nc.sync.dma_start(out=out_0[P * m : P * (m + 1), :], in_=tanh_cy[:])
+            nc.sync.dma_start(out=out_1[P * m : P * (m + 1), :], in_=tanh_cy[:])
 
         units = [(m, gate) for gate in (GATE_F, GATE_I, GATE_G) for m in (0, 1)]
         units += [(m, gate) for m in (2, 3) for gate in (GATE_F, GATE_I, GATE_G)]
@@ -433,8 +443,9 @@ def tile_layernormdropoutlstmcell_kernel(
         quantise_rows(0)
         quantise_rows(1)
         turn_norm_rows()
-        spread_norm_rows(GATE_F)
-        keep_norm_rows(GATE_F)
+        for k in (GATE_F, NORM_CY):
+            spread_norm_rows(k)
+            keep_norm_rows(k)
         for unit in units[:MATMULS_AHEAD]:
             gate_matmuls(unit)
 
@@ -446,14 +457,14 @@ def tile_layernormdropoutlstmcell_kernel(
             unit = units[step] if 0 <= step < len(units) else None
             return unit if unit and unit[1] in TURNED else None
 
-        early_rows = {6: NORM_CY, 10: GATE_O}
+        early_rows = {}
         late_rows = {2: 2, 3: 3}
 
         PRODUCT_AFTER_STATS = 3
         hidden_step = {}
         for m in range(ROW_TILES):
             hidden_step[m] = max(
-                step_of[(m, GATE_G)] + PRODUCT_AFTER_STATS + 6, step_of[(m, GATE_O)] + ACT_AFTER_SUMS + 1
+                step_of[(m, GATE_G)] + PRODUCT_AFTER_STATS + 6, step_of[(m, GATE_O)] + PRODUCT_AFTER_STATS + 1
             )
 
         for step in range(max([hidden_step[m] for m in range(ROW_TILES)]) + 1):
@@ -465,8 +476,6 @@ def tile_layernormdropoutlstmcell_kernel(
                 variance_filter(plain_at(step - 2), "%d_%d" % plain_at(step - 2))
             if 2 in due:
                 cell_mean(due[2])
-            if 3 in due:
-                variance_filter(due[3], "cy%d" % due[3])
 
             longs, smalls = [], []
             if turned_at(step):
@@ -480,6 +489,7 @@ def tile_layernormdropoutlstmcell_kernel(
             if plain_at(step - 2):
                 smalls.append((inverse_std, (plain_at(step - 2), "%d_%d" % plain_at(step - 2))))
             if 3 in due:
+                smalls.append((variance_filter, (due[3], "cy%d" % due[3])))
                 smalls.append((inverse_std, (due[3], "cy%d" % due[3])))
             if plain_at(step - 1):
                 longs.append((gate_times_gamma, (plain_at(step - 1), 0)))
@@ -517,6 +527,8 @@ def tile_layernormdropoutlstmcell_kernel(
                 gate_sums(plain_at(step))
             if turned_at(step - 1):
                 turned_normalise(turned_at(step - 1))
+            if 2 in due:
+                cell_squares(due[2])
             if plain_at(step - 1):
                 gate_squares(plain_at(step - 1))
             if plain_at(step):
@@ -525,8 +537,6 @@ def tile_layernormdropoutlstmcell_kernel(
                 turned_activation(turned_at(step - 2))
             if plain_at(step - ACT_AFTER_SUMS):
                 gate_activation(plain_at(step - ACT_AFTER_SUMS))
-            if 2 in due:
-                cell_squares(due[2])
             if 5 in due:
                 cell_tanh(due[5])
             if step - 1 in late_rows:
@@ -538,6 +548,9 @@ def tile_layernormdropoutlstmcell_kernel(
                 turned_transpose(turned_at(step - 1))
             if 0 in due:
                 cell_product_back(due[0])
+            for m in range(ROW_TILES):
+                if step == step_of[(m, GATE_O)] + PRODUCT_AFTER_STATS:
+                    out_gate_back(m)
             if step in early_rows:
                 spread_norm_rows(early_rows[step])
             if step in late_rows:

@@ -426,8 +426,8 @@ def tile_layernormdropoutlstmcell_kernel(
             for h in range(2):
                 cols = slice(BANK * h, BANK * (h + 1))
                 nc.vector.tensor_tensor(out=tanh_cy[:, cols], in0=tanh_cy[:, cols], in1=out_gate[m][:, cols], op=ALU.mult)
-            nc.sync.dma_start(out=out_0[P * m : P * (m + 1), :], in_=tanh_cy[:])
-            nc.sync.dma_start(out=out_1[P * m : P * (m + 1), :], in_=tanh_cy[:])
+                nc.sync.dma_start(out=out_0[P * m : P * (m + 1), cols], in_=tanh_cy[:, cols])
+                nc.sync.dma_start(out=out_1[P * m : P * (m + 1), cols], in_=tanh_cy[:, cols])
 
         units = [(m, gate) for gate in (GATE_F, GATE_I, GATE_G) for m in (0, 1)]
         units += [(m, gate) for m in (2, 3) for gate in (GATE_F, GATE_I, GATE_G)]
@@ -518,10 +518,10 @@ def tile_layernormdropoutlstmcell_kernel(
             if step - 2 in late_rows:
                 longs.append((quantise_rows, (late_rows[step - 2],)))
             for position in range(max(len(longs), len(smalls))):
-                if position < len(longs):
-                    longs[position][0](*longs[position][1])
                 if position < len(smalls):
                     smalls[position][0](*smalls[position][1])
+                if position < len(longs):
+                    longs[position][0](*longs[position][1])
 
             if plain_at(step):
                 gate_sums(plain_at(step))

@@ -430,7 +430,7 @@ def tile_layernormdropoutlstmcell_kernel(
                 nc.sync.dma_start(out=out_1[P * m : P * (m + 1), cols], in_=tanh_cy[:, cols])
 
         units = [(m, gate) for gate in (GATE_F, GATE_I, GATE_G) for m in (0, 1)]
-        units += [(m, gate) for m in (2, 3) for gate in (GATE_F, GATE_I, GATE_G)]
+        units += [(2, GATE_F), (2, GATE_I), (3, GATE_F), (2, GATE_G), (3, GATE_I), (3, GATE_G)]
         units += [(m, GATE_O) for m in range(ROW_TILES)]
         step_of = {}
         for step, unit in enumerate(units):
@@ -523,18 +523,18 @@ def tile_layernormdropoutlstmcell_kernel(
                 if position < len(longs):
                     longs[position][0](*longs[position][1])
 
-            if plain_at(step):
-                gate_sums(plain_at(step))
+            if turned_at(step - 2):
+                turned_activation(turned_at(step - 2))
             if turned_at(step - 1):
                 turned_normalise(turned_at(step - 1))
+            if plain_at(step):
+                gate_sums(plain_at(step))
             if 2 in due:
                 cell_squares(due[2])
             if plain_at(step - 1):
                 gate_squares(plain_at(step - 1))
             if plain_at(step):
                 gate_mean(plain_at(step))
-            if turned_at(step - 2):
-                turned_activation(turned_at(step - 2))
             if plain_at(step - ACT_AFTER_SUMS):
                 gate_activation(plain_at(step - ACT_AFTER_SUMS))
             if 5 in due:

@@ -55,7 +55,7 @@ def tile_layernormdropoutlstmcell_kernel(
         stage = ctx.enter_context(tc.tile_pool(name="stage", bufs=2))
         work = ctx.enter_context(tc.tile_pool(name="work", bufs=3))
         small = ctx.enter_context(tc.tile_pool(name="small", bufs=8))
-        psum = ctx.enter_context(tc.psum_pool(name="psum", bufs=4))
+        psum = ctx.enter_context(tc.psum_pool(name="psum", bufs=8))
         ctx.enter_context(tc.manual_schedule())
 
         one = const.tile([P, 1], F32, name="one")
@@ -78,6 +78,7 @@ def tile_layernormdropoutlstmcell_kernel(
             nc.sync.dma_start(out=xh[pair][:, :, 1, :], in_=hx[rows, :].rearrange("(j p) k -> p j k", p=P))
 
         load_rows(0)
+        load_rows(1)
 
         norm_rows = const.tile([P, HIDDEN], BF16, name="norm_rows")
         nc.vector.memset(norm_rows[:], 0.0)
@@ -109,7 +110,6 @@ def tile_layernormdropoutlstmcell_kernel(
         cx_sb = const.tile([P, ROW_TILES, HIDDEN], BF16, name="cx_sb")
         load_gate(GATE_F)
         load_gate(GATE_I)
-        load_rows(1)
         load_gate(GATE_G)
         nc.sync.dma_start(out=cx_sb[:], in_=cx.rearrange("(m p) k -> p m k", p=P))
         load_gate(GATE_O)
@@ -122,11 +122,11 @@ def tile_layernormdropoutlstmcell_kernel(
 
         def transpose_rows(m):
             words = xh[m // 2][:, m % 2, :, :].rearrange("p o k -> p (o k)").bitcast(F32)
-            flipped[m] = psum.tile([P, 2 * PASSES, P], F32, tag="slot", name="flipped%d" % m)
+            flipped[m] = [psum.tile([P, PASSES, P], F32, tag="slot", name="flipped%d_%d" % (m, b)) for b in range(2)]
             for c in range(PASSES):
                 for u in range(2):
                     nc.tensor.transpose(
-                        flipped[m][:, 2 * c + u, :],
+                        flipped[m][c // 2][:, 2 * (c % 2) + u, :],
                         words[:, 256 * c + u : 256 * (c + 1) : 2],
                         ident_f32[:],
                     )
@@ -135,7 +135,7 @@ def tile_layernormdropoutlstmcell_kernel(
             if bank == 0:
                 grouped[m] = stage.tile([P, PASSES * K_PASS], BF16, tag="grouped", name="grouped%d" % m, align_bytes=64)
             grouped_words = grouped[m][:].bitcast(F32).rearrange("p (c b u) -> p c b u", c=PASSES, u=2)
-            turned_words = flipped[m][:, 4 * bank : 4 * bank + 4, :].rearrange("p (c u) b -> p c b u", u=2)
+            turned_words = flipped[m][bank][:].rearrange("p (c u) b -> p c b u", u=2)
             if bank == 0:
                 nc.vector.tensor_copy(out=grouped_words[:, 0:2], in_=turned_words)
             else:
@@ -151,12 +151,12 @@ def tile_layernormdropoutlstmcell_kernel(
         spread = {}
 
         def spread_norm_rows(k):
-            spread[k] = psum.tile([P, 2, HIDDEN], BF16, tag="slot", name="spread%d" % k)
+            spread[k] = [psum.tile([P, HIDDEN], BF16, tag="slot", name="spread%d_%d" % (k, which)) for which in range(2)]
             for which, row, picker in ((0, k, ident_x32), (1, 5 + k, ident_bf16)):
                 for h in range(2):
                     cols = slice(BANK * h, BANK * (h + 1))
                     nc.tensor.matmul(
-                        out=spread[k][:, which, cols],
+                        out=spread[k][which][:, cols],
                         lhsT=picker[:, row : row + 1].to_broadcast([P, P]),
                         rhs=norm_rows[:, cols],
                         start=True,
@@ -164,8 +164,8 @@ def tile_layernormdropoutlstmcell_kernel(
                     )
 
         def keep_norm_rows(k):
-            nc.vector.tensor_copy(out=gamma_bc[k][:], in_=spread[k][:, 0, :])
-            nc.vector.tensor_copy(out=beta_bc[k][:], in_=spread[k][:, 1, :])
+            nc.vector.tensor_copy(out=gamma_bc[k][:], in_=spread[k][0][:])
+            nc.vector.tensor_copy(out=beta_bc[k][:], in_=spread[k][1][:])
 
         norm_cols = const.tile([P, COLUMN_TILES, 10], F32, name="norm_cols")
 
@@ -199,12 +199,12 @@ def tile_layernormdropoutlstmcell_kernel(
 
         def gate_matmuls(unit):
             m, gate = unit
-            acc[unit] = psum.tile([P, HIDDEN], F32, tag="slot", name="acc_%d_%d" % unit)
+            acc[unit] = [psum.tile([P, BANK], F32, tag="slot", name="acc_%d_%d_%d" % (unit[0], unit[1], h)) for h in range(2)]
             for c in range(PASSES):
                 for h in range(2):
                     cols = slice(HIDDEN * gate + BANK * h, HIDDEN * gate + BANK * (h + 1))
                     nc.tensor.matmul_mx(
-                        out=acc[unit][:, BANK * h : BANK * (h + 1)],
+                        out=acc[unit][h][:],
                         lhsT=x_codes[m][:, P * c : P * (c + 1)].bitcast(FP8X4),
                         lhsT_scale=x_planes[m][:, P * c : P * (c + 1)],
                         rhs=w_words[c][:, cols].bitcast(FP8X4),
@@ -221,7 +221,7 @@ def tile_layernormdropoutlstmcell_kernel(
                 cols = slice(BANK * h, BANK * (h + 1))
                 nc.scalar.activation(
                     out=raw[unit][:, cols],
-                    in_=acc[unit][:, cols],
+                    in_=acc[unit][h][:],
                     func=ACT.Identity,
                     accum_out=sums[unit][:, h : h + 1],
                 )
@@ -250,7 +250,7 @@ def tile_layernormdropoutlstmcell_kernel(
             cols = slice(BANK * h, BANK * (h + 1))
             nc.vector.scalar_tensor_tensor(
                 out=gate_act[unit][:, cols],
-                in0=acc[unit][:, cols],
+                in0=acc[unit][h][:],
                 scalar=neg_mean[unit][:],
                 in1=gamma_bc[unit[1]][:, cols],
                 op0=ALU.add,
@@ -277,7 +277,7 @@ def tile_layernormdropoutlstmcell_kernel(
         def turned_stats(unit):
             stats[unit] = small.tile([P, 2, 6], F32, tag="stats", name="stats_%d_%d" % unit)
             for h in range(2):
-                nc.vector.bn_stats(out=stats[unit][:, h, :], in_=acc[unit][:, BANK * h : BANK * (h + 1)])
+                nc.vector.bn_stats(out=stats[unit][:, h, :], in_=acc[unit][h][:])
 
         def turned_aggregate(unit):
             mean_var[unit] = small.tile([P, 2], F32, tag="mean_var", name="mean_var_%d_%d" % unit)
@@ -314,17 +314,18 @@ def tile_layernormdropoutlstmcell_kernel(
                 cols = slice(BANK * h, BANK * (h + 1))
                 nc.scalar.activation(
                     out=normal[unit][:, cols],
-                    in_=acc[unit][:, cols],
+                    in_=acc[unit][h][:],
                     func=ACT.Identity,
                     scale=rstd[unit][:],
                     bias=bias[unit][:],
                 )
 
         def turned_transpose(unit):
-            turned[unit] = psum.tile([P, HIDDEN], F32, tag="slot", name="turned_%d_%d" % unit)
+            turned[unit] = [psum.tile([P, BANK], F32, tag="slot", name="turned_%d_%d_%d" % (unit[0], unit[1], h)) for h in range(2)]
             for j in range(COLUMN_TILES):
-                cols = slice(P * j, P * (j + 1))
-                nc.tensor.transpose(turned[unit][:, cols], normal[unit][:, cols], ident_f32[:])
+                nc.tensor.transpose(
+                    turned[unit][j // 4][:, P * (j % 4) : P * (j % 4 + 1)], normal[unit][:, P * j : P * (j + 1)], ident_f32[:]
+                )
 
         def turned_activation(unit):
             gate = unit[1]
@@ -333,7 +334,7 @@ def tile_layernormdropoutlstmcell_kernel(
                 cols = slice(P * j, P * (j + 1))
                 nc.scalar.activation(
                     out=gate_act[unit][:, cols],
-                    in_=turned[unit][:, cols],
+                    in_=turned[unit][j // 4][:, P * (j % 4) : P * (j % 4 + 1)],
                     func=ACT.Tanh if gate == GATE_G else ACT.Sigmoid,
                     scale=norm_cols[:, j, gate : gate + 1],
                     bias=norm_cols[:, j, 5 + gate : 6 + gate],
@@ -350,10 +351,11 @@ def tile_layernormdropoutlstmcell_kernel(
             nc.vector.tensor_tensor(out=gate_i[:], in0=gate_i[:], in1=gate_g[:], op=ALU.mult)
 
         def cell_product_back(m):
-            product[m] = psum.tile([P, HIDDEN], F32, tag="slot", name="product%d" % m)
+            product[m] = [psum.tile([P, BANK], F32, tag="slot", name="product%d_%d" % (m, h)) for h in range(2)]
             for j in range(COLUMN_TILES):
-                cols = slice(P * j, P * (j + 1))
-                nc.tensor.transpose(product[m][:, cols], gate_act[(m, GATE_I)][:, cols], ident_f32[:])
+                nc.tensor.transpose(
+                    product[m][j // 4][:, P * (j % 4) : P * (j % 4 + 1)], gate_act[(m, GATE_I)][:, P * j : P * (j + 1)], ident_f32[:]
+                )
 
         def cell_sum(m, h):
             if h == 0:
@@ -364,7 +366,7 @@ def tile_layernormdropoutlstmcell_kernel(
                 out=gate_f[:, cols],
                 in0=gate_f[:, cols],
                 scalar=1.0,
-                in1=product[m][:, cols],
+                in1=product[m][h][:],
                 op0=ALU.mult,
                 op1=ALU.add,
                 accum_out=total[m][:, h : h + 1],
@@ -416,32 +418,34 @@ def tile_layernormdropoutlstmcell_kernel(
         out_gate = {}
 
         def out_gate_back(m):
-            out_gate[m] = psum.tile([P, HIDDEN], F32, tag="slot", name="out_gate%d" % m)
+            out_gate[m] = [psum.tile([P, BANK], F32, tag="slot", name="out_gate%d_%d" % (m, h)) for h in range(2)]
             for j in range(COLUMN_TILES):
-                cols = slice(P * j, P * (j + 1))
-                nc.tensor.transpose(out_gate[m][:, cols], gate_act[(m, GATE_O)][:, cols], ident_f32[:])
+                nc.tensor.transpose(
+                    out_gate[m][j // 4][:, P * (j % 4) : P * (j % 4 + 1)], gate_act[(m, GATE_O)][:, P * j : P * (j + 1)], ident_f32[:]
+                )
 
         def hidden_state(m):
             tanh_cy = gate_act[(m, GATE_G)]
             for h in range(2):
                 cols = slice(BANK * h, BANK * (h + 1))
-                nc.vector.tensor_tensor(out=tanh_cy[:, cols], in0=tanh_cy[:, cols], in1=out_gate[m][:, cols], op=ALU.mult)
+                nc.vector.tensor_tensor(out=tanh_cy[:, cols], in0=tanh_cy[:, cols], in1=out_gate[m][h][:], op=ALU.mult)
                 nc.sync.dma_start(out=out_0[P * m : P * (m + 1), cols], in_=tanh_cy[:, cols])
                 nc.sync.dma_start(out=out_1[P * m : P * (m + 1), cols], in_=tanh_cy[:, cols])
 
-        units = [(m, gate) for gate in (GATE_F, GATE_I, GATE_G) for m in (0, 1)]
-        units += [(2, GATE_F), (2, GATE_I), (3, GATE_F), (2, GATE_G), (3, GATE_I), (3, GATE_G)]
+        units = [(0, GATE_F), (1, GATE_F), (0, GATE_I), (2, GATE_F), (1, GATE_I), (0, GATE_G), (1, GATE_G)]
+        units += [(2, GATE_I), (3, GATE_F), (2, GATE_G), (3, GATE_I), (3, GATE_G)]
         units += [(m, GATE_O) for m in range(ROW_TILES)]
         step_of = {}
         for step, unit in enumerate(units):
             step_of[unit] = step
 
-        for m in (0, 1):
+        for m in range(ROW_TILES):
             transpose_rows(m)
             keep_rows(m, 0)
             keep_rows(m, 1)
-        quantise_rows(0)
-        quantise_rows(1)
+            if m > 0:
+                quantise_rows(m - 1)
+        quantise_rows(ROW_TILES - 1)
         turn_norm_rows()
         for k in (GATE_F, NORM_CY):
             spread_norm_rows(k)
@@ -458,7 +462,7 @@ def tile_layernormdropoutlstmcell_kernel(
             return unit if unit and unit[1] in TURNED else None
 
         early_rows = {}
-        late_rows = {2: 2, 3: 3}
+        late_rows = {}
 
         PRODUCT_AFTER_STATS = 3
         hidden_step = {}

@@ -521,6 +521,10 @@ def tile_layernormdropoutlstmcell_kernel(
                 longs.append((keep_rows, (late_rows[step - 1], 0)))
             if step - 2 in late_rows:
                 longs.append((quantise_rows, (late_rows[step - 2],)))
+            if step >= len(units):
+                for small_step, arguments in smalls:
+                    small_step(*arguments)
+                smalls = []
             for position in range(max(len(longs), len(smalls))):
                 if position < len(smalls):
                     smalls[position][0](*smalls[position][1])

@@ -465,10 +465,11 @@ def tile_layernormdropoutlstmcell_kernel(
         late_rows = {}
 
         PRODUCT_AFTER_STATS = 3
+        OUT_GATE_BACK_AFTER_STATS = 2
         hidden_step = {}
         for m in range(ROW_TILES):
             hidden_step[m] = max(
-                step_of[(m, GATE_G)] + PRODUCT_AFTER_STATS + 6, step_of[(m, GATE_O)] + PRODUCT_AFTER_STATS + 1
+                step_of[(m, GATE_G)] + PRODUCT_AFTER_STATS + 6, step_of[(m, GATE_O)] + OUT_GATE_BACK_AFTER_STATS + 1
             )
 
         for step in range(max([hidden_step[m] for m in range(ROW_TILES)]) + 1):
@@ -557,7 +558,7 @@ def tile_layernormdropoutlstmcell_kernel(
             if 0 in due:
                 cell_product_back(due[0])
             for m in range(ROW_TILES):
-                if step == step_of[(m, GATE_O)] + PRODUCT_AFTER_STATS:
+                if step == step_of[(m, GATE_O)] + OUT_GATE_BACK_AFTER_STATS:
                     out_gate_back(m)
             if step in early_rows:
                 spread_norm_rows(early_rows[step])

@@ -26,6 +26,7 @@ ROOT_HIDDEN = 32.0
 GATE_I, GATE_F, GATE_G, GATE_O, NORM_CY = 0, 1, 2, 3, 4
 GATE_ORDER = (GATE_F, GATE_I, GATE_G, GATE_O)
 TURNED = (GATE_I, GATE_G, GATE_O)
+TURNED_F_TILES = (3,)
 COLUMN_TILES = HIDDEN // P
 
 MATMULS_AHEAD = 1
@@ -174,6 +175,8 @@ def tile_layernormdropoutlstmcell_kernel(
             for j in range(COLUMN_TILES):
                 nc.tensor.transpose(turned_rows[:, j, :], norm_rows[:, P * j : P * (j + 1)], ident_bf16[:])
             nc.vector.tensor_copy(out=norm_cols[:], in_=turned_rows[:, :, 0:10])
+            beta_f = norm_cols[:, :, 5 + GATE_F : 6 + GATE_F]
+            nc.vector.tensor_scalar(out=beta_f, in0=beta_f, scalar1=1.0, scalar2=None, op0=ALU.add)
 
         acc, raw, sums, neg_mean, sum_sq, filt, rstd, gate_act = {}, {}, {}, {}, {}, {}, {}, {}
 
@@ -340,9 +343,23 @@ def tile_layernormdropoutlstmcell_kernel(
                     bias=norm_cols[:, j, 5 + gate : 6 + gate],
                 )
 
+        forget = {}
+
+        def forget_back(m):
+            forget[m] = [psum.tile([P, BANK], F32, tag="slot", name="forget%d_%d" % (m, h)) for h in range(2)]
+            for j in range(COLUMN_TILES):
+                nc.tensor.transpose(
+                    forget[m][j // 4][:, P * (j % 4) : P * (j % 4 + 1)], gate_act[(m, GATE_F)][:, P * j : P * (j + 1)], ident_f32[:]
+                )
+
         def forget_times_cx(m):
             gate_f = gate_act[(m, GATE_F)]
-            nc.vector.tensor_tensor(out=gate_f[:], in0=gate_f[:], in1=cx_sb[:, m, :], op=ALU.mult)
+            if m in TURNED_F_TILES:
+                for h in range(2):
+                    cols = slice(BANK * h, BANK * (h + 1))
+                    nc.vector.tensor_tensor(out=gate_f[:, cols], in0=cx_sb[:, m, cols], in1=forget[m][h][:], op=ALU.mult)
+            else:
+                nc.vector.tensor_tensor(out=gate_f[:], in0=gate_f[:], in1=cx_sb[:, m, :], op=ALU.mult)
 
         total, product = {}, {}
 
@@ -453,24 +470,26 @@ def tile_layernormdropoutlstmcell_kernel(
         for unit in units[:MATMULS_AHEAD]:
             gate_matmuls(unit)
 
+        def is_turned(unit):
+            return unit[1] in TURNED or (unit[1] == GATE_F and unit[0] in TURNED_F_TILES)
+
         def plain_at(step):
             unit = units[step] if 0 <= step < len(units) else None
-            return unit if unit and unit[1] not in TURNED else None
+            return unit if unit and not is_turned(unit) else None
 
         def turned_at(step):
             unit = units[step] if 0 <= step < len(units) else None
-            return unit if unit and unit[1] in TURNED else None
+            return unit if unit and is_turned(unit) else None
 
         early_rows = {}
         late_rows = {}
 
         PRODUCT_AFTER_STATS = 3
-        OUT_GATE_BACK_AFTER_STATS = 2
-        hidden_step = {}
+        BACK_AFTER_STATS = 2
+        hidden_step, forget_step = {}, {}
         for m in range(ROW_TILES):
-            hidden_step[m] = max(
-                step_of[(m, GATE_G)] + PRODUCT_AFTER_STATS + 6, step_of[(m, GATE_O)] + OUT_GATE_BACK_AFTER_STATS + 1
-            )
+            hidden_step[m] = max(step_of[(m, GATE_G)] + PRODUCT_AFTER_STATS + 6, step_of[(m, GATE_O)] + BACK_AFTER_STATS + 1)
+            forget_step[m] = step_of[(m, GATE_F)] + (BACK_AFTER_STATS if m in TURNED_F_TILES else ACT_AFTER_SUMS) + 1
 
         for step in range(max([hidden_step[m] for m in range(ROW_TILES)]) + 1):
             due = {}
@@ -505,7 +524,7 @@ def tile_layernormdropoutlstmcell_kernel(
             if plain_at(step - 3):
                 longs.append((gate_plus_beta, (plain_at(step - 3),)))
             for m in range(ROW_TILES):
-                if step == step_of[(m, GATE_F)] + ACT_AFTER_SUMS + 1:
+                if step == forget_step[m]:
                     longs.append((forget_times_cx, (m,)))
             if 0 in due:
                 longs.append((cell_product, (due[0],)))
@@ -558,8 +577,10 @@ def tile_layernormdropoutlstmcell_kernel(
             if 0 in due:
                 cell_product_back(due[0])
             for m in range(ROW_TILES):
-                if step == step_of[(m, GATE_O)] + OUT_GATE_BACK_AFTER_STATS:
+                if step == step_of[(m, GATE_O)] + BACK_AFTER_STATS:
                     out_gate_back(m)
+                if m in TURNED_F_TILES and step == step_of[(m, GATE_F)] + BACK_AFTER_STATS:
+                    forget_back(m)
             if step in early_rows:
                 spread_norm_rows(early_rows[step])
             if step in late_rows:

@@ -443,11 +443,16 @@ def tile_layernormdropoutlstmcell_kernel(
 
         def hidden_state(m):
             tanh_cy = gate_act[(m, GATE_G)]
+            rows = slice(P * m, P * (m + 1))
             for h in range(2):
                 cols = slice(BANK * h, BANK * (h + 1))
                 nc.vector.tensor_tensor(out=tanh_cy[:, cols], in0=tanh_cy[:, cols], in1=out_gate[m][h][:], op=ALU.mult)
-                nc.sync.dma_start(out=out_0[P * m : P * (m + 1), cols], in_=tanh_cy[:, cols])
-                nc.sync.dma_start(out=out_1[P * m : P * (m + 1), cols], in_=tanh_cy[:, cols])
+                if m == ROW_TILES - 1:
+                    nc.sync.dma_start(out=out_0[rows, cols], in_=tanh_cy[:, cols])
+                    nc.sync.dma_start(out=out_1[rows, cols], in_=tanh_cy[:, cols])
+            if m < ROW_TILES - 1:
+                nc.sync.dma_start(out=out_0[rows, :], in_=tanh_cy[:])
+                nc.sync.dma_start(out=out_1[rows, :], in_=tanh_cy[:])
 
         units = [(0, GATE_F), (1, GATE_F), (0, GATE_I), (2, GATE_F), (1, GATE_I), (0, GATE_G), (1, GATE_G)]
         units += [(2, GATE_I), (3, GATE_F), (2, GATE_G), (3, GATE_I), (3, GATE_G)]

@@ -501,16 +501,15 @@ def tile_layernormdropoutlstmcell_kernel(
             for m in range(ROW_TILES):
                 due[step - step_of[(m, GATE_G)] - PRODUCT_AFTER_STATS] = m
 
-            if plain_at(step - 2):
-                variance_filter(plain_at(step - 2), "%d_%d" % plain_at(step - 2))
-            if 2 in due:
-                cell_mean(due[2])
-
             longs, smalls = [], []
             if turned_at(step):
                 turned_stats(turned_at(step))
             if turned_at(step - 1):
                 turned_bias(turned_at(step - 1))
+            if plain_at(step - 2):
+                variance_filter(plain_at(step - 2), "%d_%d" % plain_at(step - 2))
+            if 2 in due:
+                cell_mean(due[2])
             if turned_at(step):
                 smalls.append((turned_aggregate, (turned_at(step),)))
                 smalls.append((turned_filter, (turned_at(step),)))

@@ -260,10 +260,11 @@ def tile_layernormdropoutlstmcell_kernel(
                 op1=ALU.mult,
             )
 
-        def gate_plus_beta(unit):
+        def gate_plus_beta(unit, h):
             act = gate_act[unit]
+            cols = slice(BANK * h, BANK * (h + 1))
             nc.vector.scalar_tensor_tensor(
-                out=act[:], in0=act[:], scalar=rstd[unit][:], in1=beta_bc[unit[1]][:], op0=ALU.mult, op1=ALU.add
+                out=act[:, cols], in0=act[:, cols], scalar=rstd[unit][:], in1=beta_bc[unit[1]][:, cols], op0=ALU.mult, op1=ALU.add
             )
 
         def gate_activation(unit):
@@ -352,20 +353,20 @@ def tile_layernormdropoutlstmcell_kernel(
                     forget[m][j // 4][:, P * (j % 4) : P * (j % 4 + 1)], gate_act[(m, GATE_F)][:, P * j : P * (j + 1)], ident_f32[:]
                 )
 
-        def forget_times_cx(m):
+        def forget_times_cx(m, h):
             gate_f = gate_act[(m, GATE_F)]
+            cols = slice(BANK * h, BANK * (h + 1))
             if m in TURNED_F_TILES:
-                for h in range(2):
-                    cols = slice(BANK * h, BANK * (h + 1))
-                    nc.vector.tensor_tensor(out=gate_f[:, cols], in0=cx_sb[:, m, cols], in1=forget[m][h][:], op=ALU.mult)
+                nc.vector.tensor_tensor(out=gate_f[:, cols], in0=cx_sb[:, m, cols], in1=forget[m][h][:], op=ALU.mult)
             else:
-                nc.vector.tensor_tensor(out=gate_f[:], in0=gate_f[:], in1=cx_sb[:, m, :], op=ALU.mult)
+                nc.vector.tensor_tensor(out=gate_f[:, cols], in0=gate_f[:, cols], in1=cx_sb[:, m, cols], op=ALU.mult)
 
         total, product = {}, {}
 
-        def cell_product(m):
+        def cell_product(m, h):
             gate_i, gate_g = gate_act[(m, GATE_I)], gate_act[(m, GATE_G)]
-            nc.vector.tensor_tensor(out=gate_i[:], in0=gate_i[:], in1=gate_g[:], op=ALU.mult)
+            cols = slice(BANK * h, BANK * (h + 1))
+            nc.vector.tensor_tensor(out=gate_i[:, cols], in0=gate_i[:, cols], in1=gate_g[:, cols], op=ALU.mult)
 
         def cell_product_back(m):
             product[m] = [psum.tile([P, BANK], F32, tag="slot", name="product%d_%d" % (m, h)) for h in range(2)]
@@ -402,12 +403,13 @@ def tile_layernormdropoutlstmcell_kernel(
                 accum_out=neg_mean[m][:],
             )
 
-        def cell_times_gamma(m):
+        def cell_times_gamma(m, h):
+            cols = slice(BANK * h, BANK * (h + 1))
             nc.vector.scalar_tensor_tensor(
-                out=gate_act[(m, GATE_I)][:],
-                in0=gate_act[(m, GATE_F)][:],
+                out=gate_act[(m, GATE_I)][:, cols],
+                in0=gate_act[(m, GATE_F)][:, cols],
                 scalar=neg_mean[m][:],
-                in1=gamma_bc[NORM_CY][:],
+                in1=gamma_bc[NORM_CY][:, cols],
                 op0=ALU.add,
                 op1=ALU.mult,
             )
@@ -422,12 +424,14 @@ def tile_layernormdropoutlstmcell_kernel(
                 accum_out=sum_sq[m][:],
             )
 
-        def cell_norm(m):
+        def cell_norm(m, h):
             cy = gate_act[(m, GATE_I)]
+            cols = slice(BANK * h, BANK * (h + 1))
             nc.vector.scalar_tensor_tensor(
-                out=cy[:], in0=cy[:], scalar=rstd[m][:], in1=beta_bc[NORM_CY][:], op0=ALU.mult, op1=ALU.add
+                out=cy[:, cols], in0=cy[:, cols], scalar=rstd[m][:], in1=beta_bc[NORM_CY][:, cols], op0=ALU.mult, op1=ALU.add
             )
-            nc.sync.dma_start(out=out_2[P * m : P * (m + 1), :], in_=cy[:])
+            if h == 1:
+                nc.sync.dma_start(out=out_2[P * m : P * (m + 1), :], in_=cy[:])
 
         def cell_tanh(m):
             nc.scalar.activation(out=gate_act[(m, GATE_G)][:], in_=gate_act[(m, GATE_I)][:], func=ACT.Tanh)
@@ -525,17 +529,22 @@ def tile_layernormdropoutlstmcell_kernel(
             if 1 in due:
                 longs.append((cell_sum, (due[1], 0)))
                 longs.append((cell_sum, (due[1], 1)))
-            if plain_at(step - 3):
-                longs.append((gate_plus_beta, (plain_at(step - 3),)))
+            for h in range(2):
+                if plain_at(step - 3):
+                    longs.append((gate_plus_beta, (plain_at(step - 3), h)))
             for m in range(ROW_TILES):
-                if step == forget_step[m]:
-                    longs.append((forget_times_cx, (m,)))
-            if 0 in due:
-                longs.append((cell_product, (due[0],)))
-            if 2 in due:
-                longs.append((cell_times_gamma, (due[2],)))
-            if 4 in due:
-                longs.append((cell_norm, (due[4],)))
+                for h in range(2):
+                    if step == forget_step[m]:
+                        longs.append((forget_times_cx, (m, h)))
+            for h in range(2):
+                if 0 in due:
+                    longs.append((cell_product, (due[0], h)))
+            for h in range(2):
+                if 2 in due:
+                    longs.append((cell_times_gamma, (due[2], h)))
+            for h in range(2):
+                if 4 in due:
+                    longs.append((cell_norm, (due[4], h)))
             for m in range(ROW_TILES):
                 if step == hidden_step[m]:
                     longs.append((hidden_state, (m,)))

@@ -86,15 +86,17 @@ def tile_layernormdropoutlstmcell_kernel(
         nc.sync.dma_start(out=norm_rows[0:5, :], in_=gamma)
         nc.sync.dma_start(out=norm_rows[5:10, :], in_=beta)
 
-        w_planes = const.tile([P, 4 * HIDDEN], U8, name="w_planes", align_bytes=64)
-        nc.vector.memset(w_planes[:].bitcast(I32), 0)
-        for w, scales in enumerate((weight_ih_scales, weight_hh_scales)):
+        w_planes = [const.tile([P, 4 * HIDDEN], U8, name="w_planes%d" % w, align_bytes=64) for w in range(2)]
+
+        def load_scales(w):
             for quad in range(4):
-                first = 32 * quad + 8 * w
                 nc.sync.dma_start(
-                    out=w_planes[first : first + 8, :].bitcast(I32),
-                    in_=scales[:, 4 * quad : 4 * quad + 4, :].bitcast(I32),
+                    out=w_planes[w][32 * quad : 32 * quad + 8, :].bitcast(I32),
+                    in_=(weight_ih_scales, weight_hh_scales)[w][:, 4 * quad : 4 * quad + 4, :].bitcast(I32),
                 )
+
+        for w in range(2):
+            nc.vector.memset(w_planes[w][:].bitcast(I32), 0)
 
         w_words = [const.tile([P, 4 * HIDDEN], I32, name="w_words%d" % c, align_bytes=64) for c in range(PASSES)]
         w_dram = [
@@ -103,17 +105,20 @@ def tile_layernormdropoutlstmcell_kernel(
             for g in range(2)
         ]
 
-        def load_gate(gate):
+        def load_gate(gate, passes):
             cols = slice(HIDDEN * gate, HIDDEN * (gate + 1))
-            for c in range(PASSES):
+            for c in passes:
                 nc.sync.dma_start(out=w_words[c][:, cols], in_=w_dram[c][:, cols])
 
         cx_sb = const.tile([P, ROW_TILES, HIDDEN], BF16, name="cx_sb")
-        load_gate(GATE_F)
-        load_gate(GATE_I)
-        load_gate(GATE_G)
+        load_scales(0)
+        load_gate(GATE_F, (0, 1))
+        load_scales(1)
+        load_gate(GATE_F, (2, 3))
+        load_gate(GATE_I, range(PASSES))
+        load_gate(GATE_G, range(PASSES))
         nc.sync.dma_start(out=cx_sb[:], in_=cx.rearrange("(m p) k -> p m k", p=P))
-        load_gate(GATE_O)
+        load_gate(GATE_O, range(PASSES))
 
         nc.vector.tensor_scalar(out=ident_x32[:], in0=ident_bf16[:], scalar1=ROOT_HIDDEN, scalar2=None, op0=ALU.mult)
 
@@ -211,7 +216,7 @@ def tile_layernormdropoutlstmcell_kernel(
                         lhsT=x_codes[m][:, P * c : P * (c + 1)].bitcast(FP8X4),
                         lhsT_scale=x_planes[m][:, P * c : P * (c + 1)],
                         rhs=w_words[c][:, cols].bitcast(FP8X4),
-                        rhs_scale=w_planes[4 * c : P, cols],
+                        rhs_scale=w_planes[c // 2][4 * (c % 2) : P, cols],
                         start=(c == 0),
                         stop=(c == PASSES - 1),
                     )

from contextlib import ExitStack

import concourse.mybir as mybir
from concourse.masks import make_identity

F32 = mybir.dt.float32
BF16 = mybir.dt.bfloat16
I32 = mybir.dt.int32
U32 = mybir.dt.uint32
U8 = mybir.dt.uint8
FP8X4 = mybir.dt.float8_e4m3fn_x4
ALU = mybir.AluOpType
ACT = mybir.ActivationFunctionType

P = 128
BATCH = 512
HIDDEN = 1024
BANK = 512
K_PASS = 512
PASSES = 4
ROW_TILES = BATCH // P
EPS = 1e-12
VAR_FILTER = 0.01
ROOT_HIDDEN = 32.0

GATE_I, GATE_F, GATE_G, GATE_O, NORM_CY = 0, 1, 2, 3, 4
GATE_ORDER = (GATE_F, GATE_I, GATE_G, GATE_O)
TURNED = (GATE_I, GATE_G, GATE_O)
TURNED_F_TILES = (3,)
COLUMN_TILES = HIDDEN // P

MATMULS_AHEAD = 1
ACT_AFTER_SUMS = 4

FLOPS = 2 * BATCH * (2 * HIDDEN) * (4 * HIDDEN)


def tile_layernormdropoutlstmcell_kernel(
    tc,
    x,
    hx,
    cx,
    weight_ih_words,
    weight_ih_scales,
    weight_hh_words,
    weight_hh_scales,
    gamma,
    beta,
    out_0,
    out_1,
    out_2,
):
    nc = tc.nc
    with ExitStack() as ctx:
        const = ctx.enter_context(tc.tile_pool(name="const", bufs=1))
        stage = ctx.enter_context(tc.tile_pool(name="stage", bufs=2))
        work = ctx.enter_context(tc.tile_pool(name="work", bufs=3))
        small = ctx.enter_context(tc.tile_pool(name="small", bufs=8))
        psum = ctx.enter_context(tc.psum_pool(name="psum", bufs=8))
        ctx.enter_context(tc.manual_schedule())

        one = const.tile([P, 1], F32, name="one")
        nc.vector.memset(one[:], 1.0)
        neg_half = const.tile([P, 1], F32, name="neg_half")
        nc.vector.memset(neg_half[:], -0.5)
        warm = const.tile([P, 1], F32, name="warm")
        nc.scalar.activation(out=warm[:], in_=one[:], func=ACT.Sigmoid)
        ident_f32 = const.tile([P, P], F32, name="ident_f32")
        make_identity(nc, ident_f32[:])
        ident_bf16 = const.tile([P, P], BF16, name="ident_bf16")
        make_identity(nc, ident_bf16[:])
        ident_x32 = const.tile([P, P], BF16, name="ident_x32")

        xh = [const.tile([P, 2, 2, HIDDEN], BF16, name="xh%d" % pair) for pair in range(2)]

        def load_rows(pair):
            rows = slice(2 * P * pair, 2 * P * (pair + 1))
            nc.sync.dma_start(out=xh[pair][:, :, 0, :], in_=x[rows, :].rearrange("(j p) k -> p j k", p=P))
            nc.sync.dma_start(out=xh[pair][:, :, 1, :], in_=hx[rows, :].rearrange("(j p) k -> p j k", p=P))

        load_rows(0)
        load_rows(1)

        norm_rows = const.tile([P, HIDDEN], BF16, name="norm_rows")
        nc.vector.memset(norm_rows[:], 0.0)
        nc.sync.dma_start(out=norm_rows[0:5, :], in_=gamma)
        nc.sync.dma_start(out=norm_rows[5:10, :], in_=beta)

        w_planes = [const.tile([P, 4 * HIDDEN], U8, name="w_planes%d" % w, align_bytes=64) for w in range(2)]

        def load_scales(w):
            for quad in range(4):
                nc.sync.dma_start(
                    out=w_planes[w][32 * quad : 32 * quad + 8, :].bitcast(I32),
                    in_=(weight_ih_scales, weight_hh_scales)[w][:, 4 * quad : 4 * quad + 4, :].bitcast(I32),
                )

        for w in range(2):
            nc.vector.memset(w_planes[w][:].bitcast(I32), 0)

        w_words = [const.tile([P, 4 * HIDDEN], I32, name="w_words%d" % c, align_bytes=64) for c in range(PASSES)]
        w_dram = [
            words[g].rearrange("p n t -> p (n t)").bitcast(I32)
            for words in (weight_ih_words, weight_hh_words)
            for g in range(2)
        ]

        def load_gate(gate, passes):
            cols = slice(HIDDEN * gate, HIDDEN * (gate + 1))
            for c in passes:
                nc.sync.dma_start(out=w_words[c][:, cols], in_=w_dram[c][:, cols])

        cx_sb = const.tile([P, ROW_TILES, HIDDEN], BF16, name="cx_sb")
        load_scales(0)
        load_gate(GATE_F, (0, 1))
        load_scales(1)
        load_gate(GATE_F, (2, 3))
        load_gate(GATE_I, range(PASSES))
        load_gate(GATE_G, range(PASSES))
        nc.sync.dma_start(out=cx_sb[:], in_=cx.rearrange("(m p) k -> p m k", p=P))
        load_gate(GATE_O, range(PASSES))

        nc.vector.tensor_scalar(out=ident_x32[:], in0=ident_bf16[:], scalar1=ROOT_HIDDEN, scalar2=None, op0=ALU.mult)

        x_codes = [const.tile([P, PASSES * P], U32, name="x_codes%d" % m, align_bytes=64) for m in range(ROW_TILES)]
        x_planes = [const.tile([P, PASSES * P], U8, name="x_planes%d" % m, align_bytes=64) for m in range(ROW_TILES)]
        grouped, flipped = {}, {}

        def transpose_rows(m):
            words = xh[m // 2][:, m % 2, :, :].rearrange("p o k -> p (o k)").bitcast(F32)
            flipped[m] = [psum.tile([P, PASSES, P], F32, tag="slot", name="flipped%d_%d" % (m, b)) for b in range(2)]
            for c in range(PASSES):
                for u in range(2):
                    nc.tensor.transpose(
                        flipped[m][c // 2][:, 2 * (c % 2) + u, :],
                        words[:, 256 * c + u : 256 * (c + 1) : 2],
                        ident_f32[:],
                    )

        def keep_rows(m, bank):
            if bank == 0:
                grouped[m] = stage.tile([P, PASSES * K_PASS], BF16, tag="grouped", name="grouped%d" % m, align_bytes=64)
            grouped_words = grouped[m][:].bitcast(F32).rearrange("p (c b u) -> p c b u", c=PASSES, u=2)
            turned_words = flipped[m][bank][:].rearrange("p (c u) b -> p c b u", u=2)
            if bank == 0:
                nc.vector.tensor_copy(out=grouped_words[:, 0:2], in_=turned_words)
            else:
                nc.scalar.copy(out=grouped_words[:, 2:4], in_=turned_words)

        def quantise_rows(m):
            nc.vector.quantize_mx(out=x_codes[m][:].bitcast(FP8X4), scales=x_planes[m][:], in_=grouped[m][:])

        gamma_bc, beta_bc = {}, {}
        for k in (GATE_F, NORM_CY):
            gamma_bc[k] = const.tile([P, HIDDEN], BF16, name="gamma_bc%d" % k)
            beta_bc[k] = const.tile([P, HIDDEN], BF16, name="beta_bc%d" % k)
        spread = {}

        def spread_norm_rows(k):
            spread[k] = [psum.tile([P, HIDDEN], BF16, tag="slot", name="spread%d_%d" % (k, which)) for which in range(2)]
            for which, row, picker in ((0, k, ident_x32), (1, 5 + k, ident_bf16)):
                for h in range(2):
                    cols = slice(BANK * h, BANK * (h + 1))
                    nc.tensor.matmul(
                        out=spread[k][which][:, cols],
                        lhsT=picker[:, row : row + 1].to_broadcast([P, P]),
                        rhs=norm_rows[:, cols],
                        start=True,
                        stop=True,
                    )

        def keep_norm_rows(k):
            nc.vector.tensor_copy(out=gamma_bc[k][:], in_=spread[k][0][:])
            nc.vector.tensor_copy(out=beta_bc[k][:], in_=spread[k][1][:])

        norm_cols = const.tile([P, COLUMN_TILES, 10], F32, name="norm_cols")

        def turn_norm_rows():
            turned_rows = psum.tile([P, COLUMN_TILES, P], BF16, tag="slot", name="turned_rows")
            for j in range(COLUMN_TILES):
                nc.tensor.transpose(turned_rows[:, j, :], norm_rows[:, P * j : P * (j + 1)], ident_bf16[:])
            nc.vector.tensor_copy(out=norm_cols[:], in_=turned_rows[:, :, 0:10])
            beta_f = norm_cols[:, :, 5 + GATE_F : 6 + GATE_F]
            nc.vector.tensor_scalar(out=beta_f, in0=beta_f, scalar1=1.0, scalar2=None, op0=ALU.add)

        acc, raw, sums, neg_mean, sum_sq, filt, rstd, gate_act = {}, {}, {}, {}, {}, {}, {}, {}

        def variance_filter(key, name):
            filt[key] = small.tile([P, 1], F32, tag="filt", name="filt_" + name)
            nc.vector.tensor_scalar(
                out=filt[key][:],
                in0=sum_sq[key][:],
                scalar1=EPS * HIDDEN,
                scalar2=VAR_FILTER * HIDDEN,
                op0=ALU.is_lt,
                op1=ALU.mult,
            )

        def inverse_std(key, name):
            padded = small.tile([P, 1], F32, tag="padded", name="padded_" + name)
            nc.vector.scalar_tensor_tensor(
                out=padded[:], in0=filt[key][:], scalar=EPS * HIDDEN, in1=sum_sq[key][:], op0=ALU.add, op1=ALU.add
            )
            rstd[key] = small.tile([P, 1], F32, tag="rstd", name="rstd_" + name)
            nc.gpsimd.tensor_tensor(out=rstd[key][:], in0=padded[:], in1=neg_half[:], op=ALU.pow)


        def gate_matmuls(unit):
            m, gate = unit
            acc[unit] = [psum.tile([P, BANK], F32, tag="slot", name="acc_%d_%d_%d" % (unit[0], unit[1], h)) for h in range(2)]
            for c in range(PASSES):
                for h in range(2):
                    cols = slice(HIDDEN * gate + BANK * h, HIDDEN * gate + BANK * (h + 1))
                    nc.tensor.matmul_mx(
                        out=acc[unit][h][:],
                        lhsT=x_codes[m][:, P * c : P * (c + 1)].bitcast(FP8X4),
                        lhsT_scale=x_planes[m][:, P * c : P * (c + 1)],
                        rhs=w_words[c][:, cols].bitcast(FP8X4),
                        rhs_scale=w_planes[c // 2][4 * (c % 2) : P, cols],
                        start=(c == 0),
                        stop=(c == PASSES - 1),
                    )

        def gate_sums(unit):
            name = "%d_%d" % unit
            raw[unit] = work.tile([P, HIDDEN], F32, tag="raw", name="raw_" + name)
            sums[unit] = small.tile([P, 2], F32, tag="sums", name="sums_" + name)
            for h in range(2):
                cols = slice(BANK * h, BANK * (h + 1))
                nc.scalar.activation(
                    out=raw[unit][:, cols],
                    in_=acc[unit][h][:],
                    func=ACT.Identity,
                    accum_out=sums[unit][:, h : h + 1],
                )

        def gate_mean(unit):
            name = "%d_%d" % unit
            scaled = small.tile([P, 2], F32, tag="scaled", name="scaled_" + name)
            neg_mean[unit] = small.tile([P, 1], F32, tag="neg_mean", name="neg_mean_" + name)
            nc.scalar.activation(
                out=scaled[:], in_=sums[unit][:], func=ACT.Identity, scale=-1.0 / HIDDEN, accum_out=neg_mean[unit][:]
            )

        def gate_squares(unit):
            sum_sq[unit] = small.tile([P, 1], F32, tag="sum_sq", name="sum_sq_%d_%d" % unit)
            nc.scalar.activation(
                out=raw[unit][:],
                in_=raw[unit][:],
                func=ACT.Square,
                bias=neg_mean[unit][:],
                accum_out=sum_sq[unit][:],
            )

        def gate_times_gamma(unit, h):
            if h == 0:
                gate_act[unit] = const.tile([P, HIDDEN], F32, name="act_%d_%d" % unit)
            cols = slice(BANK * h, BANK * (h + 1))
            nc.vector.scalar_tensor_tensor(
                out=gate_act[unit][:, cols],
                in0=acc[unit][h][:],
                scalar=neg_mean[unit][:],
                in1=gamma_bc[unit[1]][:, cols],
                op0=ALU.add,
                op1=ALU.mult,
            )

        def gate_plus_beta(unit, h):
            act = gate_act[unit]
            cols = slice(BANK * h, BANK * (h + 1))
            nc.vector.scalar_tensor_tensor(
                out=act[:, cols], in0=act[:, cols], scalar=rstd[unit][:], in1=beta_bc[unit[1]][:, cols], op0=ALU.mult, op1=ALU.add
            )

        def gate_activation(unit):
            act = gate_act[unit]
            if unit[1] == GATE_G:
                nc.scalar.activation(out=act[:], in_=act[:], func=ACT.Tanh)
            elif unit[1] == GATE_F:
                nc.scalar.activation(out=act[:], in_=act[:], func=ACT.Sigmoid, bias=one[:])
            else:
                nc.scalar.activation(out=act[:], in_=act[:], func=ACT.Sigmoid)

        stats, mean_var, bias, normal, turned = {}, {}, {}, {}, {}

        def turned_stats(unit):
            stats[unit] = small.tile([P, 2, 6], F32, tag="stats", name="stats_%d_%d" % unit)
            for h in range(2):
                nc.vector.bn_stats(out=stats[unit][:, h, :], in_=acc[unit][h][:])

        def turned_aggregate(unit):
            mean_var[unit] = small.tile([P, 2], F32, tag="mean_var", name="mean_var_%d_%d" % unit)
            nc.vector.bn_aggr(out=mean_var[unit][:], in_=stats[unit][:].rearrange("p h s -> p (h s)"))

        def turned_filter(unit):
            filt[unit] = small.tile([P, 1], F32, tag="filt", name="filt_%d_%d" % unit)
            nc.vector.tensor_scalar(
                out=filt[unit][:],
                in0=mean_var[unit][:, 1:2],
                scalar1=EPS,
                scalar2=VAR_FILTER,
                op0=ALU.is_lt,
                op1=ALU.mult,
            )

        def turned_inverse_std(unit):
            padded = small.tile([P, 1], F32, tag="padded", name="padded_%d_%d" % unit)
            nc.vector.scalar_tensor_tensor(
                out=padded[:], in0=filt[unit][:], scalar=EPS, in1=mean_var[unit][:, 1:2], op0=ALU.add, op1=ALU.add
            )
            rstd[unit] = small.tile([P, 1], F32, tag="rstd", name="rstd_%d_%d" % unit)
            nc.gpsimd.tensor_tensor(out=rstd[unit][:], in0=padded[:], in1=neg_half[:], op=ALU.pow)

        def turned_bias(unit):
            bias[unit] = small.tile([P, 1], F32, tag="bias", name="bias_%d_%d" % unit)
            nc.vector.scalar_tensor_tensor(
                out=bias[unit][:], in0=mean_var[unit][:, 0:1], scalar=-1.0, in1=rstd[unit][:], op0=ALU.mult, op1=ALU.mult
            )

        def turned_normalise(unit):
            normal[unit] = work.tile([P, HIDDEN], F32, tag="normal", name="normal_%d_%d" % unit)
            for h in range(2):
                cols = slice(BANK * h, BANK * (h + 1))
                nc.scalar.activation(
                    out=normal[unit][:, cols],
                    in_=acc[unit][h][:],
                    func=ACT.Identity,
                    scale=rstd[unit][:],
                    bias=bias[unit][:],
                )

        def turned_transpose(unit):
            turned[unit] = [psum.tile([P, BANK], F32, tag="slot", name="turned_%d_%d_%d" % (unit[0], unit[1], h)) for h in range(2)]
            for j in range(COLUMN_TILES):
                nc.tensor.transpose(
                    turned[unit][j // 4][:, P * (j % 4) : P * (j % 4 + 1)], normal[unit][:, P * j : P * (j + 1)], ident_f32[:]
                )

        def turned_activation(unit):
            gate = unit[1]
            gate_act[unit] = const.tile([P, HIDDEN], F32, name="act_%d_%d" % unit)
            for j in range(COLUMN_TILES):
                cols = slice(P * j, P * (j + 1))
                nc.scalar.activation(
                    out=gate_act[unit][:, cols],
                    in_=turned[unit][j // 4][:, P * (j % 4) : P * (j % 4 + 1)],
                    func=ACT.Tanh if gate == GATE_G else ACT.Sigmoid,
                    scale=norm_cols[:, j, gate : gate + 1],
                    bias=norm_cols[:, j, 5 + gate : 6 + gate],
                )

        forget = {}

        def forget_back(m):
            forget[m] = [psum.tile([P, BANK], F32, tag="slot", name="forget%d_%d" % (m, h)) for h in range(2)]
            for j in range(COLUMN_TILES):
                nc.tensor.transpose(
                    forget[m][j // 4][:, P * (j % 4) : P * (j % 4 + 1)], gate_act[(m, GATE_F)][:, P * j : P * (j + 1)], ident_f32[:]
                )

        def forget_times_cx(m, h):
            gate_f = gate_act[(m, GATE_F)]
            cols = slice(BANK * h, BANK * (h + 1))
            if m in TURNED_F_TILES:
                nc.vector.tensor_tensor(out=gate_f[:, cols], in0=cx_sb[:, m, cols], in1=forget[m][h][:], op=ALU.mult)
            else:
                nc.vector.tensor_tensor(out=gate_f[:, cols], in0=gate_f[:, cols], in1=cx_sb[:, m, cols], op=ALU.mult)

        total, product = {}, {}

        def cell_product(m, h):
            gate_i, gate_g = gate_act[(m, GATE_I)], gate_act[(m, GATE_G)]
            cols = slice(BANK * h, BANK * (h + 1))
            nc.vector.tensor_tensor(out=gate_i[:, cols], in0=gate_i[:, cols], in1=gate_g[:, cols], op=ALU.mult)

        def cell_product_back(m):
            product[m] = [psum.tile([P, BANK], F32, tag="slot", name="product%d_%d" % (m, h)) for h in range(2)]
            for j in range(COLUMN_TILES):
                nc.tensor.transpose(
                    product[m][j // 4][:, P * (j % 4) : P * (j % 4 + 1)], gate_act[(m, GATE_I)][:, P * j : P * (j + 1)], ident_f32[:]
                )

        def cell_sum(m, h):
            if h == 0:
                total[m] = small.tile([P, 2], F32, tag="total", name="total_%d" % m)
            gate_f = gate_act[(m, GATE_F)]
            cols = slice(BANK * h, BANK * (h + 1))
            nc.vector.scalar_tensor_tensor(
                out=gate_f[:, cols],
                in0=gate_f[:, cols],
                scalar=1.0,
                in1=product[m][h][:],
                op0=ALU.mult,
                op1=ALU.add,
                accum_out=total[m][:, h : h + 1],
            )

        def cell_mean(m):
            scaled = small.tile([P, 2], F32, tag="scaled_cy", name="scaled_cy%d" % m)
            neg_mean[m] = small.tile([P, 1], F32, tag="neg_mean_cy", name="neg_mean_cy%d" % m)
            nc.vector.tensor_scalar(
                out=scaled[:],
                in0=total[m][:],
                scalar1=-1.0 / HIDDEN,
                scalar2=None,
                op0=ALU.mult,
                op1=ALU.add,
                accum_out=neg_mean[m][:],
            )

        def cell_times_gamma(m, h):
            cols = slice(BANK * h, BANK * (h + 1))
            nc.vector.scalar_tensor_tensor(
                out=gate_act[(m, GATE_I)][:, cols],
                in0=gate_act[(m, GATE_F)][:, cols],
                scalar=neg_mean[m][:],
                in1=gamma_bc[NORM_CY][:, cols],
                op0=ALU.add,
                op1=ALU.mult,
            )

        def cell_squares(m):
            sum_sq[m] = small.tile([P, 1], F32, tag="sum_sq", name="sum_sq_cy%d" % m)
            nc.scalar.activation(
                out=gate_act[(m, GATE_G)][:],
                in_=gate_act[(m, GATE_F)][:],
                func=ACT.Square,
                bias=neg_mean[m][:],
                accum_out=sum_sq[m][:],
            )

        def cell_norm(m, h):
            cy = gate_act[(m, GATE_I)]
            cols = slice(BANK * h, BANK * (h + 1))
            nc.vector.scalar_tensor_tensor(
                out=cy[:, cols], in0=cy[:, cols], scalar=rstd[m][:], in1=beta_bc[NORM_CY][:, cols], op0=ALU.mult, op1=ALU.add
            )
            if h == 1:
                nc.sync.dma_start(out=out_2[P * m : P * (m + 1), :], in_=cy[:])

        def cell_tanh(m):
            nc.scalar.activation(out=gate_act[(m, GATE_G)][:], in_=gate_act[(m, GATE_I)][:], func=ACT.Tanh)

        out_gate = {}

        def out_gate_back(m):
            out_gate[m] = [psum.tile([P, BANK], F32, tag="slot", name="out_gate%d_%d" % (m, h)) for h in range(2)]
            for j in range(COLUMN_TILES):
                nc.tensor.transpose(
                    out_gate[m][j // 4][:, P * (j % 4) : P * (j % 4 + 1)], gate_act[(m, GATE_O)][:, P * j : P * (j + 1)], ident_f32[:]
                )

        def hidden_state(m):
            tanh_cy = gate_act[(m, GATE_G)]
            rows = slice(P * m, P * (m + 1))
            for h in range(2):
                cols = slice(BANK * h, BANK * (h + 1))
                nc.vector.tensor_tensor(out=tanh_cy[:, cols], in0=tanh_cy[:, cols], in1=out_gate[m][h][:], op=ALU.mult)
                if m == ROW_TILES - 1:
                    nc.sync.dma_start(out=out_0[rows, cols], in_=tanh_cy[:, cols])
                    nc.sync.dma_start(out=out_1[rows, cols], in_=tanh_cy[:, cols])
            if m < ROW_TILES - 1:
                nc.sync.dma_start(out=out_0[rows, :], in_=tanh_cy[:])
                nc.sync.dma_start(out=out_1[rows, :], in_=tanh_cy[:])

        units = [(0, GATE_F), (1, GATE_F), (0, GATE_I), (2, GATE_F), (1, GATE_I), (0, GATE_G), (1, GATE_G)]
        units += [(2, GATE_I), (3, GATE_F), (2, GATE_G), (3, GATE_I), (3, GATE_G)]
        units += [(m, GATE_O) for m in range(ROW_TILES)]
        step_of = {}
        for step, unit in enumerate(units):
            step_of[unit] = step

        for m in range(ROW_TILES):
            transpose_rows(m)
            keep_rows(m, 0)
            keep_rows(m, 1)
            if m > 0:
                quantise_rows(m - 1)
        quantise_rows(ROW_TILES - 1)
        turn_norm_rows()
        for k in (GATE_F, NORM_CY):
            spread_norm_rows(k)
            keep_norm_rows(k)
        for unit in units[:MATMULS_AHEAD]:
            gate_matmuls(unit)

        def is_turned(unit):
            return unit[1] in TURNED or (unit[1] == GATE_F and unit[0] in TURNED_F_TILES)

        def plain_at(step):
            unit = units[step] if 0 <= step < len(units) else None
            return unit if unit and not is_turned(unit) else None

        def turned_at(step):
            unit = units[step] if 0 <= step < len(units) else None
            return unit if unit and is_turned(unit) else None

        early_rows = {}
        late_rows = {}

        PRODUCT_AFTER_STATS = 3
        BACK_AFTER_STATS = 2
        hidden_step, forget_step = {}, {}
        for m in range(ROW_TILES):
            hidden_step[m] = max(step_of[(m, GATE_G)] + PRODUCT_AFTER_STATS + 6, step_of[(m, GATE_O)] + BACK_AFTER_STATS + 1)
            forget_step[m] = step_of[(m, GATE_F)] + (BACK_AFTER_STATS if m in TURNED_F_TILES else ACT_AFTER_SUMS) + 1

        for step in range(max([hidden_step[m] for m in range(ROW_TILES)]) + 1):
            due = {}
            for m in range(ROW_TILES):
                due[step - step_of[(m, GATE_G)] - PRODUCT_AFTER_STATS] = m

            longs, smalls = [], []
            if turned_at(step):
                turned_stats(turned_at(step))
            if turned_at(step - 1):
                turned_bias(turned_at(step - 1))
            if plain_at(step - 2):
                variance_filter(plain_at(step - 2), "%d_%d" % plain_at(step - 2))
            if 2 in due:
                cell_mean(due[2])
            if turned_at(step):
                smalls.append((turned_aggregate, (turned_at(step),)))
                smalls.append((turned_filter, (turned_at(step),)))
                smalls.append((turned_inverse_std, (turned_at(step),)))
            if plain_at(step - 2):
                smalls.append((inverse_std, (plain_at(step - 2), "%d_%d" % plain_at(step - 2))))
            if 3 in due:
                smalls.append((variance_filter, (due[3], "cy%d" % due[3])))
                smalls.append((inverse_std, (due[3], "cy%d" % due[3])))
            if plain_at(step - 1):
                longs.append((gate_times_gamma, (plain_at(step - 1), 0)))
                longs.append((gate_times_gamma, (plain_at(step - 1), 1)))
            if 1 in due:
                longs.append((cell_sum, (due[1], 0)))
                longs.append((cell_sum, (due[1], 1)))
            for h in range(2):
                if plain_at(step - 3):
                    longs.append((gate_plus_beta, (plain_at(step - 3), h)))
            for m in range(ROW_TILES):
                for h in range(2):
                    if step == forget_step[m]:
                        longs.append((forget_times_cx, (m, h)))
            for h in range(2):
                if 0 in due:
                    longs.append((cell_product, (due[0], h)))
            for h in range(2):
                if 2 in due:
                    longs.append((cell_times_gamma, (due[2], h)))
            for h in range(2):
                if 4 in due:
                    longs.append((cell_norm, (due[4], h)))
            for m in range(ROW_TILES):
                if step == hidden_step[m]:
                    longs.append((hidden_state, (m,)))
            if step - 1 in early_rows:
                longs.append((keep_norm_rows, (early_rows[step - 1],)))
            if step - 1 in late_rows:
                longs.append((keep_rows, (late_rows[step - 1], 0)))
            if step - 2 in late_rows:
                longs.append((quantise_rows, (late_rows[step - 2],)))
            if step >= len(units):
                for small_step, arguments in smalls:
                    small_step(*arguments)
                smalls = []
            for position in range(max(len(longs), len(smalls))):
                if position < len(smalls):
                    smalls[position][0](*smalls[position][1])
                if position < len(longs):
                    longs[position][0](*longs[position][1])

            if turned_at(step - 2):
                turned_activation(turned_at(step - 2))
            if turned_at(step - 1):
                turned_normalise(turned_at(step - 1))
            if plain_at(step):
                gate_sums(plain_at(step))
            if 2 in due:
                cell_squares(due[2])
            if plain_at(step - 1):
                gate_squares(plain_at(step - 1))
            if plain_at(step):
                gate_mean(plain_at(step))
            if plain_at(step - ACT_AFTER_SUMS):
                gate_activation(plain_at(step - ACT_AFTER_SUMS))
            if 5 in due:
                cell_tanh(due[5])
            if step - 1 in late_rows:
                keep_rows(late_rows[step - 1], 1)

            if 0 <= step + MATMULS_AHEAD < len(units):
                gate_matmuls(units[step + MATMULS_AHEAD])
            if turned_at(step - 1):
                turned_transpose(turned_at(step - 1))
            if 0 in due:
                cell_product_back(due[0])
            for m in range(ROW_TILES):
                if step == step_of[(m, GATE_O)] + BACK_AFTER_STATS:
                    out_gate_back(m)
                if m in TURNED_F_TILES and step == step_of[(m, GATE_F)] + BACK_AFTER_STATS:
                    forget_back(m)
            if step in early_rows:
                spread_norm_rows(early_rows[step])
            if step in late_rows:
                transpose_rows(late_rows[step])
